import numpy as np
import ml_dtypes


def mxq(x, axis, fmt="e4m3"):
    dtype, down = {"e4m3": (ml_dtypes.float8_e4m3fn, 7), "e5m2": (ml_dtypes.float8_e5m2, 14)}[fmt]
    v = np.moveaxis(np.asarray(x, np.float32).astype(ml_dtypes.bfloat16).astype(np.float64), axis, -1)
    blocks = v.reshape(v.shape[:-1] + (-1, 32))
    amax = np.abs(blocks).max(-1, keepdims=True)
    byte = np.maximum(np.where(amax > 0, np.frexp(amax)[1] - 1 + 127, 0) - down, 1)
    scale = np.exp2(byte - 127.0)
    codes = (blocks / scale).astype(np.float32).astype(dtype).astype(np.float64)
    return np.moveaxis((codes * scale).reshape(v.shape), -1, axis)


WIDE = False


def mx_kscale(k):
    if not WIDE:
        return np.ones(k)
    levels = np.array([10, -10, 5, -5, 0])
    a = np.random.permutation(np.resize(levels, k // 512 * 4)).reshape(k // 512, 4)
    idx = np.arange(k)
    return np.exp2(a[idx // 512, idx % 128 // 32])


BF16 = ml_dtypes.bfloat16


def bf(x):
    return np.asarray(x, np.float32).astype(BF16)


def f64(x):
    return np.asarray(x).astype(np.float64)


E2M1 = np.array([0.0, 0.5, 1.0, 1.5, 2.0, 3.0, 4.0, 6.0, -0.0, -0.5, -1.0, -1.5, -2.0, -3.0, -4.0, -6.0])


def pack_weight(w, fmt):
    k, n = w.shape
    w = f64(bf(w)).reshape(k // 32, 32, n)
    amax = np.abs(w).max(1)
    if fmt == "e4m3":
        byte = np.frexp(amax)[1] - 1 + 127 - 7
    else:
        mant, ex = np.frexp(amax / 6.0)
        byte = np.where(mant > 0.5, ex, ex - 1) + 127
    byte = np.clip(np.where(amax > 0, byte, 1), 1, 254)
    scaled = (w * np.exp2(127.0 - byte)[:, None, :]).reshape(k, n).astype(np.float32)
    by_word = np.ascontiguousarray(scaled.reshape(k // 512, 128, 4, n).transpose(0, 1, 3, 2))
    if fmt == "e4m3":
        words = by_word.astype(ml_dtypes.float8_e4m3fn).view(np.uint8)
    else:
        c = by_word.astype(ml_dtypes.float4_e2m1fn).view(np.uint8) & 0xF
        words = c[..., 0::2] | (c[..., 1::2] << 4)
    return np.ascontiguousarray(words), np.ascontiguousarray(byte.astype(np.uint8).reshape(k // 512, 16, n))


def unpack_weight(words, scales, fmt):
    g, p, n, _ = words.shape
    if fmt == "e4m3":
        vals = np.ascontiguousarray(words).view(ml_dtypes.float8_e4m3fn).astype(np.float64)
    else:
        nib = np.empty((g, p, n, 4), np.uint8)
        nib[..., 0::2] = words & 0xF
        nib[..., 1::2] = words >> 4
        vals = E2M1[nib]
    vals = vals * np.repeat(np.exp2(scales.astype(np.float64) - 127.0), 8, axis=1)[..., None]
    return vals.transpose(0, 1, 3, 2).reshape(g * 512, n)


B, S, D, H = 2, 2048, 1024, 8
DH = D // H


def softmax(v, axis):
    e = np.exp(v - v.max(axis, keepdims=True))
    return e / e.sum(axis, keepdims=True)


def setup_inputs():
    s = mx_kscale(D)
    x_k = bf(np.random.standard_normal((B, S, D)) * s)
    stack = np.random.standard_normal((H, D, DH)) * 1.5 * DH ** 0.25 / np.sqrt(D) / s[:, None]
    words, scales = pack_weight(stack.reshape(-1, DH), "e4m3")
    v_heads = bf(np.random.standard_normal((B, H, S, DH)) * 2.0)
    return {"x_k": x_k, "W_K_words": words, "W_K_scales": scales, "v_heads": v_heads}


def reference(x_k, W_K_words, W_K_scales, v_heads):
    wk = unpack_weight(W_K_words, W_K_scales, "e4m3").reshape(H, D, DH)
    k = mxq(f64(x_k), 2, "e4m3")[:, None] @ wk[None]
    kt = softmax(np.swapaxes(k, -1, -2) / DH ** 0.25, -2)
    return mxq(kt, 3, "e4m3") @ mxq(f64(v_heads), 2, "e4m3")

@@ -1,0 +1,251 @@
+from contextlib import ExitStack
+
+import concourse.mybir as mybir
+from concourse.masks import make_identity
+
+F32 = mybir.dt.float32
+BF16 = mybir.dt.bfloat16
+I32 = mybir.dt.int32
+U32 = mybir.dt.uint32
+U8 = mybir.dt.uint8
+FP8X4 = mybir.dt.float8_e4m3fn_x4
+ALU = mybir.AluOpType
+ACT = mybir.ActivationFunctionType
+AXIS = mybir.AxisListType
+
+B, S, D, H, DH = 2, 2048, 1024, 8, 128
+P = 128
+PACK = 4
+K_PASS = P * PACK
+F_PASSES = D // K_PASS
+CHUNKS_PER_BATCH = S // K_PASS
+CHUNKS = B * CHUNKS_PER_BATCH
+HALF = 4
+HALVES = H // HALF
+BANKS_PER_CHUNK = HALVES * PACK
+BANKS = CHUNKS * BANKS_PER_CHUNK
+PAIR = H // PACK
+SOFTMAX_SCALE = 128.0 ** -0.25
+LOAD_AHEAD = 3
+TENSOR_LEAD = 4
+VECTOR_LEAD = 2
+
+FLOPS = 2 * B * S * D * H * DH + 2 * B * H * S * DH * DH
+
+
+def tile_mhla2_pa_t_e_kernel(tc, x_k, W_K_words, W_K_scales, v_heads, out):
+    nc = tc.nc
+    with ExitStack() as ctx:
+        ctx.enter_context(tc.manual_schedule())
+        const = ctx.enter_context(tc.tile_pool(name="const", bufs=1))
+        loads = ctx.enter_context(tc.tile_pool(name="loads", bufs=LOAD_AHEAD))
+        work = ctx.enter_context(tc.tile_pool(name="work", bufs=2))
+        small = ctx.enter_context(tc.tile_pool(name="small", bufs=8))
+        keep = ctx.enter_context(tc.tile_pool(name="keep", bufs=B))
+        psum_t = ctx.enter_context(tc.psum_pool(name="psum_t", bufs=2))
+        psum_k = ctx.enter_context(tc.psum_pool(name="psum_k", bufs=6))
+
+        x_sb, v_sb, x_codes, x_scales, v_grouped = {}, {}, {}, {}, {}
+        k_ps, shift, expo, sums = {}, {}, {}, {}
+        p_codes, p_scales, v_codes, v_scales = {}, {}, {}, {}
+
+        def load_x(chunk, j):
+            if j == 0:
+                x_sb[chunk] = loads.tile([P, PACK, D], BF16, name="x_sb")
+            b, g = divmod(chunk, CHUNKS_PER_BATCH)
+            rows = x_k[b, g * K_PASS : (g + 1) * K_PASS, :].rearrange("(p j) f -> p j f", j=PACK)
+            nc.sync.dma_start(out=x_sb[chunk][:, j, :], in_=rows[:, j, :])
+
+        def load_v(chunk):
+            v_sb[chunk] = loads.tile([P, H, PACK, DH], BF16, name="v_sb")
+            b, g = divmod(chunk, CHUNKS_PER_BATCH)
+            rows = v_heads[b, :, g * K_PASS : (g + 1) * K_PASS, :]
+            nc.sync.dma_start(out=v_sb[chunk][:], in_=rows.rearrange("h (p j) e -> p h j e", j=PACK))
+
+        def transpose_x(chunk, j):
+            x_words = x_sb[chunk][:].bitcast(F32)
+            xt = psum_t.tile([P, F_PASSES, 2, P], F32, name="xt")
+            for c in range(F_PASSES):
+                for u in range(2):
+                    nc.tensor.transpose(
+                        xt[:, c, u, :], x_words[:, j, 256 * c + u : 256 * (c + 1) : 2], ident[:]
+                    )
+            grouped = work.tile([P, F_PASSES, P, PACK], BF16, name="x_grouped", bufs=3, align_bytes=64)
+            nc.scalar.copy(out=grouped[:].bitcast(F32), in_=xt[:].rearrange("q c u t -> q c t u"))
+            return grouped
+
+        def quantise_x(chunk, j, grouped):
+            if j == 0:
+                x_codes[chunk] = work.tile([P, PACK, F_PASSES, P], U32, name="x_codes", align_bytes=64)
+                x_scales[chunk] = work.tile([P, PACK, F_PASSES, P], U8, name="x_scales", align_bytes=64)
+            nc.vector.quantize_mx(
+                out=x_codes[chunk][:, j, :, :].rearrange("q c t -> q (c t)").bitcast(FP8X4),
+                scales=x_scales[chunk][:, j, :, :].rearrange("q c t -> q (c t)"),
+                in_=grouped[:].rearrange("q c t w -> q (c t w)"),
+            )
+
+        def regroup_v(chunk, pair):
+            if pair == 0:
+                v_grouped[chunk] = work.tile([P, H, DH, PACK], BF16, name="v_grouped", align_bytes=64)
+            heads = slice(pair * PAIR, (pair + 1) * PAIR)
+            nc.scalar.copy(
+                out=v_grouped[chunk][:, heads, :, :],
+                in_=v_sb[chunk][:, heads, :, :].rearrange("p h j e -> p h e j"),
+            )
+
+        def quantise_v(chunk):
+            b, g = divmod(chunk, CHUNKS_PER_BATCH)
+            if g == 0:
+                v_codes[b] = keep.tile([P, CHUNKS_PER_BATCH, H, DH], U32, name="v_codes", align_bytes=64)
+                v_scales[b] = keep.tile([P, CHUNKS_PER_BATCH, H, DH], U8, name="v_scales", align_bytes=64)
+            nc.vector.quantize_mx(
+                out=v_codes[b][:, g, :, :].rearrange("p h e -> p (h e)").bitcast(FP8X4),
+                scales=v_scales[b][:, g, :, :].rearrange("p h e -> p (h e)"),
+                in_=v_grouped[chunk][:].rearrange("p h e j -> p (h e j)"),
+            )
+
+        def project(t):
+            chunk, n = divmod(t, BANKS_PER_CHUNK)
+            hh, j = divmod(n, PACK)
+            heads = slice(hh * HALF, (hh + 1) * HALF)
+            k_ps[t] = psum_k.tile([P, HALF, DH], F32, name="k_ps")
+            for c in range(F_PASSES):
+                nc.tensor.matmul_mx(
+                    out=k_ps[t][:].rearrange("p h d -> p (h d)"),
+                    lhsT=x_codes[chunk][:, j, c, :].bitcast(FP8X4),
+                    lhsT_scale=x_scales[chunk][:, j, c, :],
+                    rhs=w_codes[:, c, heads, :].rearrange("p h n -> p (h n)").bitcast(FP8X4),
+                    rhs_scale=w_scales[:, c, heads, :].rearrange("p h n -> p (h n)"),
+                    start=(c == 0),
+                    stop=(c == F_PASSES - 1),
+                )
+
+        def find_shift(t):
+            top = small.tile([P, HALF], F32, name="top")
+            nc.vector.tensor_reduce(out=top[:], in_=k_ps[t][:], axis=AXIS.X, op=ALU.max)
+            shift[t] = small.tile([P, HALF], F32, name="shift")
+            nc.vector.tensor_scalar(
+                out=shift[t][:], in0=top[:], scalar1=-SOFTMAX_SCALE, scalar2=None, op0=ALU.mult
+            )
+
+        def exponentials(t):
+            chunk, n = divmod(t, BANKS_PER_CHUNK)
+            hh, j = divmod(n, PACK)
+            if j == 0:
+                expo[chunk, hh] = work.tile([P, PACK, HALF, DH], F32, name="expo", bufs=3)
+                sums[chunk, hh] = small.tile([P, PACK, HALF], F32, name="sums")
+            for h in range(HALF):
+                nc.scalar.activation(
+                    out=expo[chunk, hh][:, j, h, :],
+                    in_=k_ps[t][:, h, :],
+                    func=ACT.Exp,
+                    bias=shift[t][:, h : h + 1],
+                    scale=SOFTMAX_SCALE,
+                    accum_out=sums[chunk, hh][:, j, h : h + 1],
+                )
+
+        def normalise(chunk, hh):
+            b, g = divmod(chunk, CHUNKS_PER_BATCH)
+            if g == 0 and hh == 0:
+                p_codes[b] = keep.tile([P, CHUNKS_PER_BATCH, H, DH], U32, name="p_codes", align_bytes=64)
+                p_scales[b] = keep.tile([P, CHUNKS_PER_BATCH, H, DH], U8, name="p_scales", align_bytes=64)
+            heads = slice(hh * HALF, (hh + 1) * HALF)
+            inv = small.tile([P, PACK, HALF], F32, name="inv")
+            nc.vector.reciprocal(out=inv[:], in_=sums[chunk, hh][:])
+            p_grouped = work.tile([P, HALF, DH, PACK], BF16, name="p_grouped", align_bytes=64)
+            nc.vector.tensor_tensor(
+                out=p_grouped[:],
+                in0=expo[chunk, hh][:].rearrange("p j h d -> p h d j"),
+                in1=inv[:].rearrange("p j h -> p h j").unsqueeze(2).to_broadcast([P, HALF, DH, PACK]),
+                op=ALU.mult,
+            )
+            nc.vector.quantize_mx(
+                out=p_codes[b][:, g, heads, :].rearrange("p h d -> p (h d)").bitcast(FP8X4),
+                scales=p_scales[b][:, g, heads, :].rearrange("p h d -> p (h d)"),
+                in_=p_grouped[:].rearrange("p h d j -> p (h d j)"),
+            )
+
+        def summarise(b, hh):
+            o_ps = psum_k.tile([P, HALF, DH], F32, name="k_ps")
+            for h in range(HALF):
+                head = hh * HALF + h
+                for g in range(CHUNKS_PER_BATCH):
+                    nc.tensor.matmul_mx(
+                        out=o_ps[:, h, :],
+                        lhsT=p_codes[b][:, g, head, :].bitcast(FP8X4),
+                        lhsT_scale=p_scales[b][:, g, head, :],
+                        rhs=v_codes[b][:, g, head, :].bitcast(FP8X4),
+                        rhs_scale=v_scales[b][:, g, head, :],
+                        start=(g == 0),
+                        stop=(g == CHUNKS_PER_BATCH - 1),
+                    )
+            o_sb = work.tile([P, HALF, DH], F32, name="o_sb")
+            nc.scalar.copy(out=o_sb[:], in_=o_ps[:])
+            nc.sync.dma_start(
+                out=out[b, hh * HALF : (hh + 1) * HALF, :, :].rearrange("h d e -> d h e"), in_=o_sb[:]
+            )
+
+        ident = const.tile([P, P], F32)
+        make_identity(nc, ident[:])
+        w_codes = const.tile([P, F_PASSES, H, PACK * DH], U8, align_bytes=64)
+        w_scales = const.tile([P, F_PASSES, H, DH], U8, align_bytes=64)
+        nc.vector.memset(w_scales[:].rearrange("p c h n -> p (c h n)").bitcast(I32), 0)
+        zero = const.tile([P, 1], F32)
+        one = const.tile([P, 1], F32)
+        nc.vector.memset(zero[:], 0.0)
+        nc.scalar.activation(out=one[:], in_=zero[:], func=ACT.Exp)
+
+        load_x(0, 0)
+        scale_rows = W_K_scales.bitcast(I32).rearrange("(h c) (q r) w -> c q r h w", c=F_PASSES, r=4)
+        for c in range(F_PASSES):
+            for q in range(4):
+                nc.sync.dma_start(
+                    out=w_scales[32 * q : 32 * q + 4, c, :, :].bitcast(I32), in_=scale_rows[c, q]
+                )
+        code_words = W_K_words.rearrange("g p n t -> g p (n t)").bitcast(I32)
+        code_words = code_words.rearrange("(h c) p n -> c p h n", c=F_PASSES)
+        for c in range(F_PASSES):
+            nc.sync.dma_start(out=w_codes[:, c, :, :].bitcast(I32), in_=code_words[c])
+        for j in range(1, PACK):
+            load_x(0, j)
+        load_v(0)
+        for chunk in range(1, LOAD_AHEAD):
+            for j in range(PACK):
+                load_x(chunk, j)
+            load_v(chunk)
+
+        x_grouped = {}
+        for chunk in range(-1, CHUNKS + 1):
+            following = chunk + 1
+            for n in range(BANKS_PER_CHUNK):
+                t = chunk * BANKS_PER_CHUNK + n
+                if 0 <= t + TENSOR_LEAD < BANKS:
+                    project(t + TENSOR_LEAD)
+                if 0 <= t + VECTOR_LEAD < BANKS:
+                    find_shift(t + VECTOR_LEAD)
+                if 0 <= t < BANKS:
+                    exponentials(t)
+
+                if following < CHUNKS:
+                    if 1 <= n <= PACK:
+                        quantise_x(following, n - 1, x_grouped[n - 1])
+                    if n < PACK:
+                        x_grouped[n] = transpose_x(following, n)
+                    else:
+                        regroup_v(following, n - PACK)
+                    if n == PACK and following + LOAD_AHEAD < CHUNKS:
+                        for j in range(PACK):
+                            load_x(following + LOAD_AHEAD, j)
+                    if n == BANKS_PER_CHUNK - 1 and following + LOAD_AHEAD < CHUNKS:
+                        load_v(following + LOAD_AHEAD)
+
+                if n == 0 and 0 <= chunk < CHUNKS:
+                    quantise_v(chunk)
+                if n == 1 and 0 <= chunk - 1:
+                    normalise(chunk - 1, 1)
+                if n == PACK - 1 and 0 <= chunk - 1 and chunk % CHUNKS_PER_BATCH == 0:
+                    summarise((chunk - 1) // CHUNKS_PER_BATCH, 1)
+                if n == PACK + 1 and 0 <= chunk < CHUNKS:
+                    normalise(chunk, 0)
+                if n == BANKS_PER_CHUNK - 1 and 0 <= chunk < CHUNKS and following % CHUNKS_PER_BATCH == 0:
+                    summarise(chunk // CHUNKS_PER_BATCH, 0)

@@ -27,8 +27,8 @@ BANKS = CHUNKS * BANKS_PER_CHUNK
 PAIR = H // PACK
 SOFTMAX_SCALE = 128.0 ** -0.25
 LOAD_AHEAD = 3
-TENSOR_LEAD = 4
-VECTOR_LEAD = 2
+TENSOR_LEAD = 5
+VECTOR_LEAD = 3
 
 FLOPS = 2 * B * S * D * H * DH + 2 * B * H * S * DH * DH
 
@@ -45,9 +45,10 @@ def tile_mhla2_pa_t_e_kernel(tc, x_k, W_K_words, W_K_scales, v_heads, out):
         psum_t = ctx.enter_context(tc.psum_pool(name="psum_t", bufs=2))
         psum_k = ctx.enter_context(tc.psum_pool(name="psum_k", bufs=6))
 
-        x_sb, v_sb, x_codes, x_scales, v_grouped = {}, {}, {}, {}, {}
-        k_ps, shift, expo, sums = {}, {}, {}, {}
-        p_codes, p_scales, v_codes, v_scales = {}, {}, {}, {}
+        x_sb, x_ps, x_grouped, x_codes, x_scales = {}, {}, {}, {}, {}
+        v_sb, v_grouped, v_codes, v_scales = {}, {}, {}, {}
+        k_ps, top, shift, expo, sums, inv = {}, {}, {}, {}, {}, {}
+        p_grouped, p_codes, p_scales = {}, {}, {}
 
         def load_x(chunk, j):
             if j == 0:
@@ -56,32 +57,44 @@ def tile_mhla2_pa_t_e_kernel(tc, x_k, W_K_words, W_K_scales, v_heads, out):
             rows = x_k[b, g * K_PASS : (g + 1) * K_PASS, :].rearrange("(p j) f -> p j f", j=PACK)
             nc.sync.dma_start(out=x_sb[chunk][:, j, :], in_=rows[:, j, :])
 
-        def load_v(chunk):
-            v_sb[chunk] = loads.tile([P, H, PACK, DH], BF16, name="v_sb")
+        def load_v(chunk, pair):
+            if pair == 0:
+                v_sb[chunk] = loads.tile([P, H, PACK, DH], BF16, name="v_sb")
             b, g = divmod(chunk, CHUNKS_PER_BATCH)
-            rows = v_heads[b, :, g * K_PASS : (g + 1) * K_PASS, :]
-            nc.sync.dma_start(out=v_sb[chunk][:], in_=rows.rearrange("h (p j) e -> p h j e", j=PACK))
+            heads = slice(pair * PAIR, (pair + 1) * PAIR)
+            rows = v_heads[b, heads, g * K_PASS : (g + 1) * K_PASS, :]
+            nc.sync.dma_start(
+                out=v_sb[chunk][:, heads, :, :], in_=rows.rearrange("h (p j) e -> p h j e", j=PACK)
+            )
 
         def transpose_x(chunk, j):
             x_words = x_sb[chunk][:].bitcast(F32)
-            xt = psum_t.tile([P, F_PASSES, 2, P], F32, name="xt")
+            x_ps[chunk, j] = psum_t.tile([P, F_PASSES, 2, P], F32, name="x_ps")
             for c in range(F_PASSES):
                 for u in range(2):
                     nc.tensor.transpose(
-                        xt[:, c, u, :], x_words[:, j, 256 * c + u : 256 * (c + 1) : 2], ident[:]
+                        x_ps[chunk, j][:, c, u, :],
+                        x_words[:, j, 256 * c + u : 256 * (c + 1) : 2],
+                        ident[:],
                     )
-            grouped = work.tile([P, F_PASSES, P, PACK], BF16, name="x_grouped", bufs=3, align_bytes=64)
-            nc.scalar.copy(out=grouped[:].bitcast(F32), in_=xt[:].rearrange("q c u t -> q c t u"))
-            return grouped
 
-        def quantise_x(chunk, j, grouped):
+        def copy_x(chunk, j):
+            x_grouped[chunk, j] = work.tile(
+                [P, F_PASSES, P, PACK], BF16, name="x_grouped", bufs=3, align_bytes=64
+            )
+            nc.scalar.copy(
+                out=x_grouped[chunk, j][:].bitcast(F32),
+                in_=x_ps[chunk, j][:].rearrange("q c u t -> q c t u"),
+            )
+
+        def quantise_x(chunk, j):
             if j == 0:
                 x_codes[chunk] = work.tile([P, PACK, F_PASSES, P], U32, name="x_codes", align_bytes=64)
                 x_scales[chunk] = work.tile([P, PACK, F_PASSES, P], U8, name="x_scales", align_bytes=64)
             nc.vector.quantize_mx(
                 out=x_codes[chunk][:, j, :, :].rearrange("q c t -> q (c t)").bitcast(FP8X4),
                 scales=x_scales[chunk][:, j, :, :].rearrange("q c t -> q (c t)"),
-                in_=grouped[:].rearrange("q c t w -> q (c t w)"),
+                in_=x_grouped[chunk, j][:].rearrange("q c t w -> q (c t w)"),
             )
 
         def regroup_v(chunk, pair):
@@ -93,15 +106,16 @@ def tile_mhla2_pa_t_e_kernel(tc, x_k, W_K_words, W_K_scales, v_heads, out):
                 in_=v_sb[chunk][:, heads, :, :].rearrange("p h j e -> p h e j"),
             )
 
-        def quantise_v(chunk):
+        def quantise_v(chunk, hh):
             b, g = divmod(chunk, CHUNKS_PER_BATCH)
-            if g == 0:
+            if g == 0 and hh == 0:
                 v_codes[b] = keep.tile([P, CHUNKS_PER_BATCH, H, DH], U32, name="v_codes", align_bytes=64)
                 v_scales[b] = keep.tile([P, CHUNKS_PER_BATCH, H, DH], U8, name="v_scales", align_bytes=64)
+            heads = slice(hh * HALF, (hh + 1) * HALF)
             nc.vector.quantize_mx(
-                out=v_codes[b][:, g, :, :].rearrange("p h e -> p (h e)").bitcast(FP8X4),
-                scales=v_scales[b][:, g, :, :].rearrange("p h e -> p (h e)"),
-                in_=v_grouped[chunk][:].rearrange("p h e j -> p (h e j)"),
+                out=v_codes[b][:, g, heads, :].rearrange("p h e -> p (h e)").bitcast(FP8X4),
+                scales=v_scales[b][:, g, heads, :].rearrange("p h e -> p (h e)"),
+                in_=v_grouped[chunk][:, heads, :, :].rearrange("p h e j -> p (h e j)"),
             )
 
         def project(t):
@@ -120,12 +134,14 @@ def tile_mhla2_pa_t_e_kernel(tc, x_k, W_K_words, W_K_scales, v_heads, out):
                     stop=(c == F_PASSES - 1),
                 )
 
-        def find_shift(t):
-            top = small.tile([P, HALF], F32, name="top")
-            nc.vector.tensor_reduce(out=top[:], in_=k_ps[t][:], axis=AXIS.X, op=ALU.max)
+        def find_top(t):
+            top[t] = small.tile([P, HALF], F32, name="top")
+            nc.vector.tensor_reduce(out=top[t][:], in_=k_ps[t][:], axis=AXIS.X, op=ALU.max)
+
+        def make_shift(t):
             shift[t] = small.tile([P, HALF], F32, name="shift")
             nc.vector.tensor_scalar(
-                out=shift[t][:], in0=top[:], scalar1=-SOFTMAX_SCALE, scalar2=None, op0=ALU.mult
+                out=shift[t][:], in0=top[t][:], scalar1=-SOFTMAX_SCALE, scalar2=None, op0=ALU.mult
             )
 
         def exponentials(t):
@@ -144,25 +160,30 @@ def tile_mhla2_pa_t_e_kernel(tc, x_k, W_K_words, W_K_scales, v_heads, out):
                     accum_out=sums[chunk, hh][:, j, h : h + 1],
                 )
 
-        def normalise(chunk, hh):
+        def invert_sums(chunk, hh):
+            inv[chunk, hh] = small.tile([P, PACK, HALF], F32, name="inv")
+            nc.vector.reciprocal(out=inv[chunk, hh][:], in_=sums[chunk, hh][:])
+
+        def scale_p(chunk, hh):
+            p_grouped[chunk, hh] = work.tile([P, HALF, DH, PACK], BF16, name="p_grouped", align_bytes=64)
+            inv_of_token = inv[chunk, hh][:].rearrange("p j h -> p h j").unsqueeze(2)
+            nc.vector.tensor_tensor(
+                out=p_grouped[chunk, hh][:],
+                in0=expo[chunk, hh][:].rearrange("p j h d -> p h d j"),
+                in1=inv_of_token.to_broadcast([P, HALF, DH, PACK]),
+                op=ALU.mult,
+            )
+
+        def quantise_p(chunk, hh):
             b, g = divmod(chunk, CHUNKS_PER_BATCH)
             if g == 0 and hh == 0:
                 p_codes[b] = keep.tile([P, CHUNKS_PER_BATCH, H, DH], U32, name="p_codes", align_bytes=64)
                 p_scales[b] = keep.tile([P, CHUNKS_PER_BATCH, H, DH], U8, name="p_scales", align_bytes=64)
             heads = slice(hh * HALF, (hh + 1) * HALF)
-            inv = small.tile([P, PACK, HALF], F32, name="inv")
-            nc.vector.reciprocal(out=inv[:], in_=sums[chunk, hh][:])
-            p_grouped = work.tile([P, HALF, DH, PACK], BF16, name="p_grouped", align_bytes=64)
-            nc.vector.tensor_tensor(
-                out=p_grouped[:],
-                in0=expo[chunk, hh][:].rearrange("p j h d -> p h d j"),
-                in1=inv[:].rearrange("p j h -> p h j").unsqueeze(2).to_broadcast([P, HALF, DH, PACK]),
-                op=ALU.mult,
-            )
             nc.vector.quantize_mx(
                 out=p_codes[b][:, g, heads, :].rearrange("p h d -> p (h d)").bitcast(FP8X4),
                 scales=p_scales[b][:, g, heads, :].rearrange("p h d -> p (h d)"),
-                in_=p_grouped[:].rearrange("p h d j -> p (h d j)"),
+                in_=p_grouped[chunk, hh][:].rearrange("p h d j -> p (h d j)"),
             )
 
         def summarise(b, hh):
@@ -195,57 +216,67 @@ def tile_mhla2_pa_t_e_kernel(tc, x_k, W_K_words, W_K_scales, v_heads, out):
         nc.vector.memset(zero[:], 0.0)
         nc.scalar.activation(out=one[:], in_=zero[:], func=ACT.Exp)
 
-        load_x(0, 0)
+        for j in range(PACK):
+            load_x(0, j)
+        for pair in range(PACK):
+            load_v(0, pair)
+        code_words = W_K_words.rearrange("g p n t -> g p (n t)").bitcast(I32)
+        code_words = code_words.rearrange("(h c) p n -> c p h n", c=F_PASSES)
+        for c in range(F_PASSES):
+            nc.sync.dma_start(out=w_codes[:, c, :, :].bitcast(I32), in_=code_words[c])
         scale_rows = W_K_scales.bitcast(I32).rearrange("(h c) (q r) w -> c q r h w", c=F_PASSES, r=4)
         for c in range(F_PASSES):
             for q in range(4):
                 nc.sync.dma_start(
                     out=w_scales[32 * q : 32 * q + 4, c, :, :].bitcast(I32), in_=scale_rows[c, q]
                 )
-        code_words = W_K_words.rearrange("g p n t -> g p (n t)").bitcast(I32)
-        code_words = code_words.rearrange("(h c) p n -> c p h n", c=F_PASSES)
-        for c in range(F_PASSES):
-            nc.sync.dma_start(out=w_codes[:, c, :, :].bitcast(I32), in_=code_words[c])
-        for j in range(1, PACK):
-            load_x(0, j)
-        load_v(0)
         for chunk in range(1, LOAD_AHEAD):
             for j in range(PACK):
                 load_x(chunk, j)
-            load_v(chunk)
+            for pair in range(PACK):
+                load_v(chunk, pair)
 
-        x_grouped = {}
         for chunk in range(-1, CHUNKS + 1):
             following = chunk + 1
             for n in range(BANKS_PER_CHUNK):
                 t = chunk * BANKS_PER_CHUNK + n
+                hh, phase = divmod(n, PACK)
+
+                if hh == 0 and following < CHUNKS:
+                    transpose_x(following, phase)
                 if 0 <= t + TENSOR_LEAD < BANKS:
                     project(t + TENSOR_LEAD)
+
                 if 0 <= t + VECTOR_LEAD < BANKS:
-                    find_shift(t + VECTOR_LEAD)
+                    find_top(t + VECTOR_LEAD)
+                done_chunk, done_hh = (chunk - 1, 1) if hh == 0 else (chunk, 0)
+                if phase == 0 and 0 <= chunk < CHUNKS:
+                    quantise_v(chunk, hh)
+                if phase == 1 and 0 <= done_chunk < CHUNKS:
+                    invert_sums(done_chunk, done_hh)
+                if phase == 2 and 0 <= done_chunk < CHUNKS:
+                    scale_p(done_chunk, done_hh)
+                if phase == 3 and 0 <= done_chunk < CHUNKS:
+                    quantise_p(done_chunk, done_hh)
+                if 0 <= t + VECTOR_LEAD < BANKS:
+                    make_shift(t + VECTOR_LEAD)
+
                 if 0 <= t < BANKS:
                     exponentials(t)
 
                 if following < CHUNKS:
-                    if 1 <= n <= PACK:
-                        quantise_x(following, n - 1, x_grouped[n - 1])
-                    if n < PACK:
-                        x_grouped[n] = transpose_x(following, n)
+                    if hh == 0:
+                        copy_x(following, phase)
                     else:
-                        regroup_v(following, n - PACK)
+                        regroup_v(following, phase)
+                    if 1 <= n <= PACK:
+                        quantise_x(following, n - 1)
                     if n == PACK and following + LOAD_AHEAD < CHUNKS:
                         for j in range(PACK):
                             load_x(following + LOAD_AHEAD, j)
                     if n == BANKS_PER_CHUNK - 1 and following + LOAD_AHEAD < CHUNKS:
-                        load_v(following + LOAD_AHEAD)
+                        for pair in range(PACK):
+                            load_v(following + LOAD_AHEAD, pair)
 
-                if n == 0 and 0 <= chunk < CHUNKS:
-                    quantise_v(chunk)
-                if n == 1 and 0 <= chunk - 1:
-                    normalise(chunk - 1, 1)
-                if n == PACK - 1 and 0 <= chunk - 1 and chunk % CHUNKS_PER_BATCH == 0:
-                    summarise((chunk - 1) // CHUNKS_PER_BATCH, 1)
-                if n == PACK + 1 and 0 <= chunk < CHUNKS:
-                    normalise(chunk, 0)
-                if n == BANKS_PER_CHUNK - 1 and 0 <= chunk < CHUNKS and following % CHUNKS_PER_BATCH == 0:
-                    summarise(chunk // CHUNKS_PER_BATCH, 0)
+                if phase == 0 and chunk >= 1 and chunk % CHUNKS_PER_BATCH == 0:
+                    summarise(chunk // CHUNKS_PER_BATCH - 1, hh)

@@ -29,6 +29,7 @@ SOFTMAX_SCALE = 128.0 ** -0.25
 LOAD_AHEAD = 3
 TENSOR_LEAD = 5
 VECTOR_LEAD = 3
+VECTOR_PAIRS = 2
 
 FLOPS = 2 * B * S * D * H * DH + 2 * B * H * S * DH * DH
 
@@ -101,7 +102,8 @@ def tile_mhla2_pa_t_e_kernel(tc, x_k, W_K_words, W_K_scales, v_heads, out):
             if pair == 0:
                 v_grouped[chunk] = work.tile([P, H, DH, PACK], BF16, name="v_grouped", align_bytes=64)
             heads = slice(pair * PAIR, (pair + 1) * PAIR)
-            nc.scalar.copy(
+            copy = nc.vector.tensor_copy if pair < VECTOR_PAIRS else nc.scalar.copy
+            copy(
                 out=v_grouped[chunk][:, heads, :, :],
                 in_=v_sb[chunk][:, heads, :, :].rearrange("p h j e -> p h e j"),
             )

@@ -29,7 +29,9 @@ SOFTMAX_SCALE = 128.0 ** -0.25
 LOAD_AHEAD = 3
 TENSOR_LEAD = 5
 VECTOR_LEAD = 3
-VECTOR_PAIRS = 2
+GROUPS = CHUNKS * HALVES
+VECTOR_HEADS = 1
+RUN = 4
 
 FLOPS = 2 * B * S * D * H * DH + 2 * B * H * S * DH * DH
 
@@ -98,26 +100,24 @@ def tile_mhla2_pa_t_e_kernel(tc, x_k, W_K_words, W_K_scales, v_heads, out):
                 in_=x_grouped[chunk, j][:].rearrange("q c t w -> q (c t w)"),
             )
 
-        def regroup_v(chunk, pair):
-            if pair == 0:
+        def regroup_v(chunk, head):
+            if head == 0:
                 v_grouped[chunk] = work.tile([P, H, DH, PACK], BF16, name="v_grouped", align_bytes=64)
-            heads = slice(pair * PAIR, (pair + 1) * PAIR)
-            copy = nc.vector.tensor_copy if pair < VECTOR_PAIRS else nc.scalar.copy
+            copy = nc.vector.tensor_copy if head < VECTOR_HEADS else nc.scalar.copy
             copy(
-                out=v_grouped[chunk][:, heads, :, :],
-                in_=v_sb[chunk][:, heads, :, :].rearrange("p h j e -> p h e j"),
+                out=v_grouped[chunk][:, head, :, :].rearrange("p (c i) j -> p c j i", i=RUN),
+                in_=v_sb[chunk][:, head, :, :].rearrange("p j (c i) -> p c j i", i=RUN),
             )
 
-        def quantise_v(chunk, hh):
+        def quantise_v(chunk):
             b, g = divmod(chunk, CHUNKS_PER_BATCH)
-            if g == 0 and hh == 0:
+            if g == 0:
                 v_codes[b] = keep.tile([P, CHUNKS_PER_BATCH, H, DH], U32, name="v_codes", align_bytes=64)
                 v_scales[b] = keep.tile([P, CHUNKS_PER_BATCH, H, DH], U8, name="v_scales", align_bytes=64)
-            heads = slice(hh * HALF, (hh + 1) * HALF)
             nc.vector.quantize_mx(
-                out=v_codes[b][:, g, heads, :].rearrange("p h e -> p (h e)").bitcast(FP8X4),
-                scales=v_scales[b][:, g, heads, :].rearrange("p h e -> p (h e)"),
-                in_=v_grouped[chunk][:, heads, :, :].rearrange("p h e j -> p (h e j)"),
+                out=v_codes[b][:, g, :, :].rearrange("p h e -> p (h e)").bitcast(FP8X4),
+                scales=v_scales[b][:, g, :, :].rearrange("p h e -> p (h e)"),
+                in_=v_grouped[chunk][:].rearrange("p h e j -> p (h e j)"),
             )
 
         def project(t):
@@ -142,41 +142,47 @@ def tile_mhla2_pa_t_e_kernel(tc, x_k, W_K_words, W_K_scales, v_heads, out):
 
         def make_shift(t):
             shift[t] = small.tile([P, HALF], F32, name="shift")
-            nc.vector.tensor_scalar(
-                out=shift[t][:], in0=top[t][:], scalar1=-SOFTMAX_SCALE, scalar2=None, op0=ALU.mult
+            nc.gpsimd.tensor_scalar(
+                out=shift[t][:],
+                in0=top[t][:],
+                scalar1=-SOFTMAX_SCALE,
+                scalar2=0.0,
+                op0=ALU.mult,
+                op1=ALU.add,
             )
 
         def exponentials(t):
-            chunk, n = divmod(t, BANKS_PER_CHUNK)
-            hh, j = divmod(n, PACK)
+            s, j = divmod(t, PACK)
             if j == 0:
-                expo[chunk, hh] = work.tile([P, PACK, HALF, DH], F32, name="expo", bufs=3)
-                sums[chunk, hh] = small.tile([P, PACK, HALF], F32, name="sums")
+                expo[s] = work.tile([P, PACK, HALF, DH], F32, name="expo", bufs=3)
+                sums[s] = small.tile([P, PACK, HALF], F32, name="sums")
             for h in range(HALF):
                 nc.scalar.activation(
-                    out=expo[chunk, hh][:, j, h, :],
+                    out=expo[s][:, j, h, :],
                     in_=k_ps[t][:, h, :],
                     func=ACT.Exp,
                     bias=shift[t][:, h : h + 1],
                     scale=SOFTMAX_SCALE,
-                    accum_out=sums[chunk, hh][:, j, h : h + 1],
+                    accum_out=sums[s][:, j, h : h + 1],
                 )
 
-        def invert_sums(chunk, hh):
-            inv[chunk, hh] = small.tile([P, PACK, HALF], F32, name="inv")
-            nc.vector.reciprocal(out=inv[chunk, hh][:], in_=sums[chunk, hh][:])
+        def invert_sums(s):
+            inv[s] = small.tile([P, PACK, HALF], F32, name="inv")
+            nc.vector.reciprocal(out=inv[s][:], in_=sums[s][:])
 
-        def scale_p(chunk, hh):
-            p_grouped[chunk, hh] = work.tile([P, HALF, DH, PACK], BF16, name="p_grouped", align_bytes=64)
-            inv_of_token = inv[chunk, hh][:].rearrange("p j h -> p h j").unsqueeze(2)
+        def scale_p(s, h):
+            if h == 0:
+                p_grouped[s] = work.tile([P, HALF, DH, PACK], BF16, name="p_grouped", align_bytes=64)
+            inv_of_token = inv[s][:, :, h].unsqueeze(1).unsqueeze(3)
             nc.vector.tensor_tensor(
-                out=p_grouped[chunk, hh][:],
-                in0=expo[chunk, hh][:].rearrange("p j h d -> p h d j"),
-                in1=inv_of_token.to_broadcast([P, HALF, DH, PACK]),
+                out=p_grouped[s][:, h, :, :].rearrange("p (c i) j -> p c j i", i=RUN),
+                in0=expo[s][:, :, h, :].rearrange("p j (c i) -> p c j i", i=RUN),
+                in1=inv_of_token.to_broadcast([P, DH // RUN, PACK, RUN]),
                 op=ALU.mult,
             )
 
-        def quantise_p(chunk, hh):
+        def quantise_p(s):
+            chunk, hh = divmod(s, HALVES)
             b, g = divmod(chunk, CHUNKS_PER_BATCH)
             if g == 0 and hh == 0:
                 p_codes[b] = keep.tile([P, CHUNKS_PER_BATCH, H, DH], U32, name="p_codes", align_bytes=64)
@@ -185,7 +191,7 @@ def tile_mhla2_pa_t_e_kernel(tc, x_k, W_K_words, W_K_scales, v_heads, out):
             nc.vector.quantize_mx(
                 out=p_codes[b][:, g, heads, :].rearrange("p h d -> p (h d)").bitcast(FP8X4),
                 scales=p_scales[b][:, g, heads, :].rearrange("p h d -> p (h d)"),
-                in_=p_grouped[chunk, hh][:].rearrange("p h d j -> p (h d j)"),
+                in_=p_grouped[s][:].rearrange("p h d j -> p (h d j)"),
             )
 
         def summarise(b, hh):
@@ -212,73 +218,85 @@ def tile_mhla2_pa_t_e_kernel(tc, x_k, W_K_words, W_K_scales, v_heads, out):
         make_identity(nc, ident[:])
         w_codes = const.tile([P, F_PASSES, H, PACK * DH], U8, align_bytes=64)
         w_scales = const.tile([P, F_PASSES, H, DH], U8, align_bytes=64)
-        nc.vector.memset(w_scales[:].rearrange("p c h n -> p (c h n)").bitcast(I32), 0)
+        w_scales_as_loaded = const.tile([P, H, F_PASSES, DH], U8)
+        nc.vector.memset(w_scales_as_loaded[:].rearrange("p h c n -> p (h c n)").bitcast(I32), 0)
         zero = const.tile([P, 1], F32)
         one = const.tile([P, 1], F32)
         nc.vector.memset(zero[:], 0.0)
         nc.scalar.activation(out=one[:], in_=zero[:], func=ACT.Exp)
 
-        for j in range(PACK):
-            load_x(0, j)
-        for pair in range(PACK):
-            load_v(0, pair)
         code_words = W_K_words.rearrange("g p n t -> g p (n t)").bitcast(I32)
         code_words = code_words.rearrange("(h c) p n -> c p h n", c=F_PASSES)
-        for c in range(F_PASSES):
-            nc.sync.dma_start(out=w_codes[:, c, :, :].bitcast(I32), in_=code_words[c])
-        scale_rows = W_K_scales.bitcast(I32).rearrange("(h c) (q r) w -> c q r h w", c=F_PASSES, r=4)
-        for c in range(F_PASSES):
-            for q in range(4):
+
+        def load_w_codes(hh):
+            heads = slice(hh * HALF, (hh + 1) * HALF)
+            for c in range(F_PASSES):
                 nc.sync.dma_start(
-                    out=w_scales[32 * q : 32 * q + 4, c, :, :].bitcast(I32), in_=scale_rows[c, q]
+                    out=w_codes[:, c, heads, :].bitcast(I32), in_=code_words[c][:, heads, :]
                 )
+
+        for j in range(PACK):
+            load_x(0, j)
+        load_w_codes(0)
+        scale_rows = W_K_scales.bitcast(I32).rearrange("(h c) (q r) w -> q r h c w", c=F_PASSES, r=4)
+        for q in range(4):
+            nc.sync.dma_start(
+                out=w_scales_as_loaded[32 * q : 32 * q + 4, :, :, :].bitcast(I32), in_=scale_rows[q]
+            )
+        nc.vector.tensor_copy(
+            out=w_scales[:].bitcast(I32),
+            in_=w_scales_as_loaded[:].bitcast(I32).rearrange("p h c w -> p c h w"),
+        )
+        load_w_codes(1)
+        for pair in range(PACK):
+            load_v(0, pair)
         for chunk in range(1, LOAD_AHEAD):
             for j in range(PACK):
                 load_x(chunk, j)
             for pair in range(PACK):
                 load_v(chunk, pair)
 
-        for chunk in range(-1, CHUNKS + 1):
+        for t in range(-BANKS_PER_CHUNK, BANKS + BANKS_PER_CHUNK):
+            group, phase = divmod(t, PACK)
+            chunk, hh = divmod(group, HALVES)
             following = chunk + 1
-            for n in range(BANKS_PER_CHUNK):
-                t = chunk * BANKS_PER_CHUNK + n
-                hh, phase = divmod(n, PACK)
 
-                if hh == 0 and following < CHUNKS:
-                    transpose_x(following, phase)
-                if 0 <= t + TENSOR_LEAD < BANKS:
-                    project(t + TENSOR_LEAD)
+            if hh == 0 and following < CHUNKS:
+                transpose_x(following, phase)
+            if 0 <= t + TENSOR_LEAD < BANKS:
+                project(t + TENSOR_LEAD)
 
-                if 0 <= t + VECTOR_LEAD < BANKS:
-                    find_top(t + VECTOR_LEAD)
-                done_chunk, done_hh = (chunk - 1, 1) if hh == 0 else (chunk, 0)
-                if phase == 0 and 0 <= chunk < CHUNKS:
-                    quantise_v(chunk, hh)
-                if phase == 1 and 0 <= done_chunk < CHUNKS:
-                    invert_sums(done_chunk, done_hh)
-                if phase == 2 and 0 <= done_chunk < CHUNKS:
-                    scale_p(done_chunk, done_hh)
-                if phase == 3 and 0 <= done_chunk < CHUNKS:
-                    quantise_p(done_chunk, done_hh)
-                if 0 <= t + VECTOR_LEAD < BANKS:
-                    make_shift(t + VECTOR_LEAD)
+            if phase == 1 and 0 <= group - 2 < GROUPS:
+                quantise_p(group - 2)
+            if phase == 1 and 0 <= group - 1 < GROUPS:
+                invert_sums(group - 1)
+            if 0 <= t + VECTOR_LEAD < BANKS:
+                find_top(t + VECTOR_LEAD)
+                make_shift(t + VECTOR_LEAD)
+            scaled = group - 1 if phase > 0 else group - 2
+            if 0 <= scaled < GROUPS:
+                scale_p(scaled, (phase - 1) % HALF)
+            if phase == 0 and hh == 0 and 0 <= chunk - 1:
+                quantise_v(chunk - 1)
 
-                if 0 <= t < BANKS:
-                    exponentials(t)
+            if 0 <= t < BANKS:
+                exponentials(t)
+            if hh == 0 and following < CHUNKS:
+                copy_x(following, phase)
+            if hh == 1 and 0 <= chunk < CHUNKS:
+                for head in range(phase * PAIR, (phase + 1) * PAIR):
+                    regroup_v(chunk, head)
+            if 1 <= t % BANKS_PER_CHUNK <= PACK and following < CHUNKS:
+                quantise_x(following, t % BANKS_PER_CHUNK - 1)
 
-                if following < CHUNKS:
-                    if hh == 0:
-                        copy_x(following, phase)
-                    else:
-                        regroup_v(following, phase)
-                    if 1 <= n <= PACK:
-                        quantise_x(following, n - 1)
-                    if n == PACK and following + LOAD_AHEAD < CHUNKS:
-                        for j in range(PACK):
-                            load_x(following + LOAD_AHEAD, j)
-                    if n == BANKS_PER_CHUNK - 1 and following + LOAD_AHEAD < CHUNKS:
-                        for pair in range(PACK):
-                            load_v(following + LOAD_AHEAD, pair)
+            if phase == PACK - 1 and hh == 0 and following + LOAD_AHEAD < CHUNKS:
+                for j in range(PACK):
+                    load_x(following + LOAD_AHEAD, j)
+            if phase == PACK - 1 and hh == 1 and 0 <= chunk and chunk + LOAD_AHEAD < CHUNKS:
+                for pair in range(PACK):
+                    load_v(chunk + LOAD_AHEAD, pair)
 
-                if phase == 0 and chunk >= 1 and chunk % CHUNKS_PER_BATCH == 0:
-                    summarise(chunk // CHUNKS_PER_BATCH - 1, hh)
+            if phase == 2 and 0 <= group - 2 < GROUPS:
+                summed_chunk, summed_hh = divmod(group - 2, HALVES)
+                if (summed_chunk + 1) % CHUNKS_PER_BATCH == 0:
+                    summarise(summed_chunk // CHUNKS_PER_BATCH, summed_hh)

@@ -173,11 +173,11 @@ def tile_mhla2_pa_t_e_kernel(tc, x_k, W_K_words, W_K_scales, v_heads, out):
         def scale_p(s, h):
             if h == 0:
                 p_grouped[s] = work.tile([P, HALF, DH, PACK], BF16, name="p_grouped", align_bytes=64)
-            inv_of_token = inv[s][:, :, h].unsqueeze(1).unsqueeze(3)
+            inv_of_token = inv[s][:, :, h].unsqueeze(1)
             nc.vector.tensor_tensor(
-                out=p_grouped[s][:, h, :, :].rearrange("p (c i) j -> p c j i", i=RUN),
-                in0=expo[s][:, :, h, :].rearrange("p j (c i) -> p c j i", i=RUN),
-                in1=inv_of_token.to_broadcast([P, DH // RUN, PACK, RUN]),
+                out=p_grouped[s][:, h, :, :],
+                in0=expo[s][:, :, h, :].rearrange("p j d -> p d j"),
+                in1=inv_of_token.to_broadcast([P, DH, PACK]),
                 op=ALU.mult,
             )
 

@@ -30,7 +30,6 @@ LOAD_AHEAD = 3
 TENSOR_LEAD = 5
 VECTOR_LEAD = 3
 GROUPS = CHUNKS * HALVES
-VECTOR_HEADS = 1
 RUN = 4
 
 FLOPS = 2 * B * S * D * H * DH + 2 * B * H * S * DH * DH
@@ -103,7 +102,7 @@ def tile_mhla2_pa_t_e_kernel(tc, x_k, W_K_words, W_K_scales, v_heads, out):
         def regroup_v(chunk, head):
             if head == 0:
                 v_grouped[chunk] = work.tile([P, H, DH, PACK], BF16, name="v_grouped", align_bytes=64)
-            copy = nc.vector.tensor_copy if head < VECTOR_HEADS else nc.scalar.copy
+            copy = nc.vector.tensor_copy if chunk == 0 else nc.scalar.copy
             copy(
                 out=v_grouped[chunk][:, head, :, :].rearrange("p (c i) j -> p c j i", i=RUN),
                 in_=v_sb[chunk][:, head, :, :].rearrange("p j (c i) -> p c j i", i=RUN),
@@ -173,11 +172,11 @@ def tile_mhla2_pa_t_e_kernel(tc, x_k, W_K_words, W_K_scales, v_heads, out):
         def scale_p(s, h):
             if h == 0:
                 p_grouped[s] = work.tile([P, HALF, DH, PACK], BF16, name="p_grouped", align_bytes=64)
-            inv_of_token = inv[s][:, :, h].unsqueeze(1)
+            inv_of_token = inv[s][:, :, h].unsqueeze(1).unsqueeze(3)
             nc.vector.tensor_tensor(
-                out=p_grouped[s][:, h, :, :],
-                in0=expo[s][:, :, h, :].rearrange("p j d -> p d j"),
-                in1=inv_of_token.to_broadcast([P, DH, PACK]),
+                out=p_grouped[s][:, h, :, :].rearrange("p (c i) j -> p c j i", i=RUN),
+                in0=expo[s][:, :, h, :].rearrange("p j (c i) -> p c j i", i=RUN),
+                in1=inv_of_token.to_broadcast([P, DH // RUN, PACK, RUN]),
                 op=ALU.mult,
             )
 
@@ -247,9 +246,9 @@ def tile_mhla2_pa_t_e_kernel(tc, x_k, W_K_words, W_K_scales, v_heads, out):
             out=w_scales[:].bitcast(I32),
             in_=w_scales_as_loaded[:].bitcast(I32).rearrange("p h c w -> p c h w"),
         )
-        load_w_codes(1)
         for pair in range(PACK):
             load_v(0, pair)
+        load_w_codes(1)
         for chunk in range(1, LOAD_AHEAD):
             for j in range(PACK):
                 load_x(chunk, j)
@@ -276,25 +275,25 @@ def tile_mhla2_pa_t_e_kernel(tc, x_k, W_K_words, W_K_scales, v_heads, out):
             scaled = group - 1 if phase > 0 else group - 2
             if 0 <= scaled < GROUPS:
                 scale_p(scaled, (phase - 1) % HALF)
-            if phase == 0 and hh == 0 and 0 <= chunk - 1:
-                quantise_v(chunk - 1)
+            if phase == 0 and hh == 0 and 0 <= chunk < CHUNKS:
+                quantise_v(chunk)
 
             if 0 <= t < BANKS:
                 exponentials(t)
             if hh == 0 and following < CHUNKS:
                 copy_x(following, phase)
-            if hh == 1 and 0 <= chunk < CHUNKS:
+            if hh == 1 and following < CHUNKS:
                 for head in range(phase * PAIR, (phase + 1) * PAIR):
-                    regroup_v(chunk, head)
+                    regroup_v(following, head)
             if 1 <= t % BANKS_PER_CHUNK <= PACK and following < CHUNKS:
                 quantise_x(following, t % BANKS_PER_CHUNK - 1)
 
             if phase == PACK - 1 and hh == 0 and following + LOAD_AHEAD < CHUNKS:
                 for j in range(PACK):
                     load_x(following + LOAD_AHEAD, j)
-            if phase == PACK - 1 and hh == 1 and 0 <= chunk and chunk + LOAD_AHEAD < CHUNKS:
+            if phase == PACK - 1 and hh == 1 and following + LOAD_AHEAD < CHUNKS:
                 for pair in range(PACK):
-                    load_v(chunk + LOAD_AHEAD, pair)
+                    load_v(following + LOAD_AHEAD, pair)
 
             if phase == 2 and 0 <= group - 2 < GROUPS:
                 summed_chunk, summed_hh = divmod(group - 2, HALVES)

@@ -136,19 +136,13 @@ def tile_mhla2_pa_t_e_kernel(tc, x_k, W_K_words, W_K_scales, v_heads, out):
                 )
 
         def find_top(t):
-            top[t] = small.tile([P, HALF], F32, name="top")
-            nc.vector.tensor_reduce(out=top[t][:], in_=k_ps[t][:], axis=AXIS.X, op=ALU.max)
+            if t % 2 == 0:
+                top[t // 2] = small.tile([P, 2, HALF], F32, name="top")
+            nc.vector.tensor_reduce(out=top[t // 2][:, t % 2, :], in_=k_ps[t][:], axis=AXIS.X, op=ALU.max)
 
-        def make_shift(t):
-            shift[t] = small.tile([P, HALF], F32, name="shift")
-            nc.gpsimd.tensor_scalar(
-                out=shift[t][:],
-                in0=top[t][:],
-                scalar1=-SOFTMAX_SCALE,
-                scalar2=0.0,
-                op0=ALU.mult,
-                op1=ALU.add,
-            )
+        def make_shifts(u):
+            shift[u] = small.tile([P, 2, HALF], F32, name="shift")
+            nc.scalar.mul(out=shift[u][:], in_=top[u][:], mul=-SOFTMAX_SCALE)
 
         def exponentials(t):
             s, j = divmod(t, PACK)
@@ -160,7 +154,7 @@ def tile_mhla2_pa_t_e_kernel(tc, x_k, W_K_words, W_K_scales, v_heads, out):
                     out=expo[s][:, j, h, :],
                     in_=k_ps[t][:, h, :],
                     func=ACT.Exp,
-                    bias=shift[t][:, h : h + 1],
+                    bias=shift[t // 2][:, t % 2, h : h + 1],
                     scale=SOFTMAX_SCALE,
                     accum_out=sums[s][:, j, h : h + 1],
                 )
@@ -271,7 +265,6 @@ def tile_mhla2_pa_t_e_kernel(tc, x_k, W_K_words, W_K_scales, v_heads, out):
                 invert_sums(group - 1)
             if 0 <= t + VECTOR_LEAD < BANKS:
                 find_top(t + VECTOR_LEAD)
-                make_shift(t + VECTOR_LEAD)
             scaled = group - 1 if phase > 0 else group - 2
             if 0 <= scaled < GROUPS:
                 scale_p(scaled, (phase - 1) % HALF)
@@ -280,6 +273,8 @@ def tile_mhla2_pa_t_e_kernel(tc, x_k, W_K_words, W_K_scales, v_heads, out):
 
             if 0 <= t < BANKS:
                 exponentials(t)
+            if t % 2 == 1 and 0 <= t + 1 < BANKS:
+                make_shifts((t + 1) // 2)
             if hh == 0 and following < CHUNKS:
                 copy_x(following, phase)
             if hh == 1 and following < CHUNKS:

@@ -159,15 +159,15 @@ def tile_mhla2_pa_t_e_kernel(tc, x_k, W_K_words, W_K_scales, v_heads, out):
                     accum_out=sums[s][:, j, h : h + 1],
                 )
 
-        def invert_sums(s):
-            inv[s] = small.tile([P, PACK, HALF], F32, name="inv")
-            nc.vector.reciprocal(out=inv[s][:], in_=sums[s][:])
+        def invert_sums(s, first, last):
+            inv[s, first] = small.tile([P, PACK, last - first], F32, name="inv%d" % first)
+            nc.vector.reciprocal(out=inv[s, first][:], in_=sums[s][:, :, first:last])
 
-        def scale_p(s, h):
-            if h == 0:
+        def scale_p(s, h, engine, first):
+            if s not in p_grouped:
                 p_grouped[s] = work.tile([P, HALF, DH, PACK], BF16, name="p_grouped", align_bytes=64)
-            inv_of_token = inv[s][:, :, h].unsqueeze(1).unsqueeze(3)
-            nc.vector.tensor_tensor(
+            inv_of_token = inv[s, first][:, :, h - first].unsqueeze(1).unsqueeze(3)
+            engine.tensor_tensor(
                 out=p_grouped[s][:, h, :, :].rearrange("p (c i) j -> p c j i", i=RUN),
                 in0=expo[s][:, :, h, :].rearrange("p j (c i) -> p c j i", i=RUN),
                 in1=inv_of_token.to_broadcast([P, DH // RUN, PACK, RUN]),
@@ -259,15 +259,24 @@ def tile_mhla2_pa_t_e_kernel(tc, x_k, W_K_words, W_K_scales, v_heads, out):
             if 0 <= t + TENSOR_LEAD < BANKS:
                 project(t + TENSOR_LEAD)
 
+            scaling = 0 <= group - 1 < GROUPS
+            helper = nc.gpsimd if group < GROUPS else nc.vector
+            if phase == 1 and scaling:
+                invert_sums(group - 1, 0, 3)
+                scale_p(group - 1, 2, helper, 0)
+            if phase == 3 and scaling:
+                invert_sums(group - 1, 3, 4)
+                scale_p(group - 1, 3, helper, 3)
+            if phase % 2 == 1:
+                for bank in (t + VECTOR_LEAD, t + VECTOR_LEAD + 1):
+                    if 0 <= bank < BANKS:
+                        find_top(bank)
+            if phase == 1 and scaling:
+                scale_p(group - 1, 0, nc.vector, 0)
             if phase == 1 and 0 <= group - 2 < GROUPS:
                 quantise_p(group - 2)
-            if phase == 1 and 0 <= group - 1 < GROUPS:
-                invert_sums(group - 1)
-            if 0 <= t + VECTOR_LEAD < BANKS:
-                find_top(t + VECTOR_LEAD)
-            scaled = group - 1 if phase > 0 else group - 2
-            if 0 <= scaled < GROUPS:
-                scale_p(scaled, (phase - 1) % HALF)
+            if phase == 2 and scaling:
+                scale_p(group - 1, 1, nc.vector, 0)
             if phase == 0 and hh == 0 and 0 <= chunk < CHUNKS:
                 quantise_v(chunk)
 

@@ -30,6 +30,8 @@ LOAD_AHEAD = 3
 TENSOR_LEAD = 5
 VECTOR_LEAD = 3
 GROUPS = CHUNKS * HALVES
+V_HEADS = 3
+FIRST_V = {-2: (0, 1, 2), 0: (3, 4, 5), 2: (6, 7)}
 RUN = 4
 
 FLOPS = 2 * B * S * D * H * DH + 2 * B * H * S * DH * DH
@@ -102,7 +104,7 @@ def tile_mhla2_pa_t_e_kernel(tc, x_k, W_K_words, W_K_scales, v_heads, out):
         def regroup_v(chunk, head):
             if head == 0:
                 v_grouped[chunk] = work.tile([P, H, DH, PACK], BF16, name="v_grouped", align_bytes=64)
-            copy = nc.vector.tensor_copy if chunk == 0 else nc.scalar.copy
+            copy = nc.vector.tensor_copy if chunk == 0 or head < V_HEADS else nc.scalar.copy
             copy(
                 out=v_grouped[chunk][:, head, :, :].rearrange("p (c i) j -> p c j i", i=RUN),
                 in_=v_sb[chunk][:, head, :, :].rearrange("p j (c i) -> p c j i", i=RUN),
@@ -140,24 +142,27 @@ def tile_mhla2_pa_t_e_kernel(tc, x_k, W_K_words, W_K_scales, v_heads, out):
                 top[t // 2] = small.tile([P, 2, HALF], F32, name="top")
             nc.vector.tensor_reduce(out=top[t // 2][:, t % 2, :], in_=k_ps[t][:], axis=AXIS.X, op=ALU.max)
 
-        def make_shifts(u):
-            shift[u] = small.tile([P, 2, HALF], F32, name="shift")
-            nc.scalar.mul(out=shift[u][:], in_=top[u][:], mul=-SOFTMAX_SCALE)
+        def make_shifts(u, banks):
+            shifts = small.tile([P, len(banks), HALF], F32, name="shift%d" % len(banks))
+            nc.scalar.mul(
+                out=shifts[:], in_=top[u][:, banks[0] : banks[-1] + 1, :], mul=-SOFTMAX_SCALE
+            )
+            for i, bank in enumerate(banks):
+                shift[2 * u + bank] = shifts[:, i, :]
 
-        def exponentials(t):
-            s, j = divmod(t, PACK)
-            if j == 0:
+        def exponentials(s, j, h):
+            if j == 0 and h == 0:
                 expo[s] = work.tile([P, PACK, HALF, DH], F32, name="expo", bufs=3)
                 sums[s] = small.tile([P, PACK, HALF], F32, name="sums")
-            for h in range(HALF):
-                nc.scalar.activation(
-                    out=expo[s][:, j, h, :],
-                    in_=k_ps[t][:, h, :],
-                    func=ACT.Exp,
-                    bias=shift[t // 2][:, t % 2, h : h + 1],
-                    scale=SOFTMAX_SCALE,
-                    accum_out=sums[s][:, j, h : h + 1],
-                )
+            t = s * PACK + j
+            nc.scalar.activation(
+                out=expo[s][:, j, h, :],
+                in_=k_ps[t][:, h, :],
+                func=ACT.Exp,
+                bias=shift[t][:, h : h + 1],
+                scale=SOFTMAX_SCALE,
+                accum_out=sums[s][:, j, h : h + 1],
+            )
 
         def invert_sums(s, first, last):
             inv[s, first] = small.tile([P, PACK, last - first], F32, name="inv%d" % first)
@@ -174,23 +179,23 @@ def tile_mhla2_pa_t_e_kernel(tc, x_k, W_K_words, W_K_scales, v_heads, out):
                 op=ALU.mult,
             )
 
-        def quantise_p(s):
+        def quantise_p(s, first, last):
             chunk, hh = divmod(s, HALVES)
             b, g = divmod(chunk, CHUNKS_PER_BATCH)
-            if g == 0 and hh == 0:
+            if g == 0 and hh == 0 and first == 0:
                 p_codes[b] = keep.tile([P, CHUNKS_PER_BATCH, H, DH], U32, name="p_codes", align_bytes=64)
                 p_scales[b] = keep.tile([P, CHUNKS_PER_BATCH, H, DH], U8, name="p_scales", align_bytes=64)
-            heads = slice(hh * HALF, (hh + 1) * HALF)
+            heads = slice(hh * HALF + first, hh * HALF + last)
             nc.vector.quantize_mx(
                 out=p_codes[b][:, g, heads, :].rearrange("p h d -> p (h d)").bitcast(FP8X4),
                 scales=p_scales[b][:, g, heads, :].rearrange("p h d -> p (h d)"),
-                in_=p_grouped[s][:].rearrange("p h d j -> p (h d j)"),
+                in_=p_grouped[s][:, first:last, :, :].rearrange("p h d j -> p (h d j)"),
             )
 
-        def summarise(b, hh):
-            o_ps = psum_k.tile([P, HALF, DH], F32, name="k_ps")
-            for h in range(HALF):
-                head = hh * HALF + h
+        def summarise(b, first, last):
+            o_ps = psum_k.tile([P, last - first, DH], F32, name="k_ps")
+            for h in range(last - first):
+                head = first + h
                 for g in range(CHUNKS_PER_BATCH):
                     nc.tensor.matmul_mx(
                         out=o_ps[:, h, :],
@@ -201,11 +206,9 @@ def tile_mhla2_pa_t_e_kernel(tc, x_k, W_K_words, W_K_scales, v_heads, out):
                         start=(g == 0),
                         stop=(g == CHUNKS_PER_BATCH - 1),
                     )
-            o_sb = work.tile([P, HALF, DH], F32, name="o_sb")
+            o_sb = work.tile([P, last - first, DH], F32, name="o_sb%d" % (last - first), bufs=HALF)
             nc.scalar.copy(out=o_sb[:], in_=o_ps[:])
-            nc.sync.dma_start(
-                out=out[b, hh * HALF : (hh + 1) * HALF, :, :].rearrange("h d e -> d h e"), in_=o_sb[:]
-            )
+            nc.sync.dma_start(out=out[b, first:last, :, :].rearrange("h d e -> d h e"), in_=o_sb[:])
 
         ident = const.tile([P, P], F32)
         make_identity(nc, ident[:])
@@ -236,10 +239,6 @@ def tile_mhla2_pa_t_e_kernel(tc, x_k, W_K_words, W_K_scales, v_heads, out):
             nc.sync.dma_start(
                 out=w_scales_as_loaded[32 * q : 32 * q + 4, :, :, :].bitcast(I32), in_=scale_rows[q]
             )
-        nc.vector.tensor_copy(
-            out=w_scales[:].bitcast(I32),
-            in_=w_scales_as_loaded[:].bitcast(I32).rearrange("p h c w -> p c h w"),
-        )
         for pair in range(PACK):
             load_v(0, pair)
         load_w_codes(1)
@@ -249,57 +248,83 @@ def tile_mhla2_pa_t_e_kernel(tc, x_k, W_K_words, W_K_scales, v_heads, out):
             for pair in range(PACK):
                 load_v(chunk, pair)
 
-        for t in range(-BANKS_PER_CHUNK, BANKS + BANKS_PER_CHUNK):
+        last = GROUPS - 1
+        for t in range(-BANKS_PER_CHUNK, BANKS + PACK):
             group, phase = divmod(t, PACK)
             chunk, hh = divmod(group, HALVES)
             following = chunk + 1
+            step = t % BANKS_PER_CHUNK
 
             if hh == 0 and following < CHUNKS:
                 transpose_x(following, phase)
             if 0 <= t + TENSOR_LEAD < BANKS:
                 project(t + TENSOR_LEAD)
 
-            scaling = 0 <= group - 1 < GROUPS
-            helper = nc.gpsimd if group < GROUPS else nc.vector
-            if phase == 1 and scaling:
-                invert_sums(group - 1, 0, 3)
-                scale_p(group - 1, 2, helper, 0)
-            if phase == 3 and scaling:
-                invert_sums(group - 1, 3, 4)
-                scale_p(group - 1, 3, helper, 3)
+            if 0 <= group - 1 < last:
+                if phase == 1:
+                    invert_sums(group - 1, 0, 3)
+                    scale_p(group - 1, 2, nc.gpsimd if group < last else nc.vector, 0)
+                if phase == 3:
+                    invert_sums(group - 1, 3, 4)
+                    scale_p(group - 1, 3, nc.gpsimd if group < last else nc.vector, 3)
             if phase % 2 == 1:
                 for bank in (t + VECTOR_LEAD, t + VECTOR_LEAD + 1):
                     if 0 <= bank < BANKS:
                         find_top(bank)
-            if phase == 1 and scaling:
-                scale_p(group - 1, 0, nc.vector, 0)
-            if phase == 1 and 0 <= group - 2 < GROUPS:
-                quantise_p(group - 2)
-            if phase == 2 and scaling:
-                scale_p(group - 1, 1, nc.vector, 0)
-            if phase == 0 and hh == 0 and 0 <= chunk < CHUNKS:
+            if 0 <= group - 1 < last and phase in (1, 2):
+                scale_p(group - 1, phase - 1, nc.vector, 0)
+            if phase == 1 and 0 <= group - 2 < last - 1:
+                quantise_p(group - 2, 0, HALF)
+            if step == 4 and 0 <= chunk < CHUNKS:
                 quantise_v(chunk)
+            for head in FIRST_V.get(t, ()):
+                regroup_v(0, head)
+            if step in (2, 4, 6) and 0 < following < CHUNKS:
+                regroup_v(following, step // 2 - 1)
 
-            if 0 <= t < BANKS:
-                exponentials(t)
-            if t % 2 == 1 and 0 <= t + 1 < BANKS:
-                make_shifts((t + 1) // 2)
+            if 0 <= group < last:
+                for h in range(HALF):
+                    exponentials(group, phase, h)
+            if group == last:
+                for j in range(PACK):
+                    exponentials(group, j, phase)
+            if t == -1:
+                make_shifts(0, (0,))
+                make_shifts(0, (1,))
+            elif phase % 2 == 1 and 0 <= t + 1 and group < last:
+                make_shifts((t + 1) // 2, (0, 1))
+                if group == last - 1 and phase == 3:
+                    make_shifts((t + 3) // 2, (0, 1))
             if hh == 0 and following < CHUNKS:
                 copy_x(following, phase)
-            if hh == 1 and following < CHUNKS:
-                for head in range(phase * PAIR, (phase + 1) * PAIR):
-                    regroup_v(following, head)
-            if 1 <= t % BANKS_PER_CHUNK <= PACK and following < CHUNKS:
-                quantise_x(following, t % BANKS_PER_CHUNK - 1)
+            if hh == 1 and 0 < following < CHUNKS:
+                regroup_v(following, V_HEADS + phase)
+                if phase == PACK - 1:
+                    regroup_v(following, H - 1)
+            if 1 <= step <= PACK and following < CHUNKS:
+                quantise_x(following, step - 1)
+            if t == 1 - BANKS_PER_CHUNK:
+                nc.vector.tensor_copy(
+                    out=w_scales[:].bitcast(I32),
+                    in_=w_scales_as_loaded[:].bitcast(I32).rearrange("p h c w -> p c h w"),
+                )
 
             if phase == PACK - 1 and hh == 0 and following + LOAD_AHEAD < CHUNKS:
                 for j in range(PACK):
                     load_x(following + LOAD_AHEAD, j)
-            if phase == PACK - 1 and hh == 1 and following + LOAD_AHEAD < CHUNKS:
+            if phase == PACK - 1 and hh == 0 and 0 <= chunk < CHUNKS - LOAD_AHEAD:
                 for pair in range(PACK):
-                    load_v(following + LOAD_AHEAD, pair)
+                    load_v(chunk + LOAD_AHEAD, pair)
 
-            if phase == 2 and 0 <= group - 2 < GROUPS:
+            if phase == 2 and 0 <= group - 2 < last - 1:
                 summed_chunk, summed_hh = divmod(group - 2, HALVES)
                 if (summed_chunk + 1) % CHUNKS_PER_BATCH == 0:
-                    summarise(summed_chunk // CHUNKS_PER_BATCH, summed_hh)
+                    summarise(summed_chunk // CHUNKS_PER_BATCH, summed_hh * HALF, (summed_hh + 1) * HALF)
+            if group == last + 1:
+                if phase == 0:
+                    quantise_p(last - 1, 0, HALF)
+                    summarise(B - 1, 0, HALF)
+                invert_sums(last, phase, phase + 1)
+                scale_p(last, phase, nc.vector, phase)
+                quantise_p(last, phase, phase + 1)
+                summarise(B - 1, HALF + phase, HALF + phase + 1)

@@ -30,9 +30,10 @@ LOAD_AHEAD = 3
 TENSOR_LEAD = 5
 VECTOR_LEAD = 3
 GROUPS = CHUNKS * HALVES
-V_HEADS = 3
-FIRST_V = {-2: (0, 1, 2), 0: (3, 4, 5), 2: (6, 7)}
-RUN = 4
+FIRST_V = {2: (2, 3, 4), 4: (5, 6, 7)}
+GC=96
+QX={1: (0,), 2: (1,), 3: (2,), 4: (3,)}
+RUN = 8
 
 FLOPS = 2 * B * S * D * H * DH + 2 * B * H * S * DH * DH
 
@@ -50,9 +51,9 @@ def tile_mhla2_pa_t_e_kernel(tc, x_k, W_K_words, W_K_scales, v_heads, out):
         psum_k = ctx.enter_context(tc.psum_pool(name="psum_k", bufs=6))
 
         x_sb, x_ps, x_grouped, x_codes, x_scales = {}, {}, {}, {}, {}
-        v_sb, v_grouped, v_codes, v_scales = {}, {}, {}, {}
+        v_sb, v_ps, v_grouped, v_codes, v_scales = {}, {}, {}, {}, {}
         k_ps, top, shift, expo, sums, inv = {}, {}, {}, {}, {}, {}
-        p_grouped, p_codes, p_scales = {}, {}, {}
+        p_grouped, p_codes, p_scales, o_banks = {}, {}, {}, {}
 
         def load_x(chunk, j):
             if j == 0:
@@ -101,13 +102,32 @@ def tile_mhla2_pa_t_e_kernel(tc, x_k, W_K_words, W_K_scales, v_heads, out):
                 in_=x_grouped[chunk, j][:].rearrange("q c t w -> q (c t w)"),
             )
 
-        def regroup_v(chunk, head):
-            if head == 0:
+        def regroup_v(chunk, head, copy):
+            if chunk not in v_grouped:
                 v_grouped[chunk] = work.tile([P, H, DH, PACK], BF16, name="v_grouped", align_bytes=64)
-            copy = nc.vector.tensor_copy if chunk == 0 or head < V_HEADS else nc.scalar.copy
             copy(
                 out=v_grouped[chunk][:, head, :, :].rearrange("p (c i) j -> p c j i", i=RUN),
                 in_=v_sb[chunk][:, head, :, :].rearrange("p j (c i) -> p c j i", i=RUN),
+            )
+
+        def multiply_v(chunk, pair):
+            v_ps[chunk, pair] = psum_t.tile([P, PAIR, DH * PACK], BF16, name="x_ps")
+            for i in range(PAIR):
+                nc.tensor.matmul(
+                    v_ps[chunk, pair][:, i, :],
+                    lhsT=ident_bf16[:],
+                    rhs=v_sb[chunk][:, pair * PAIR + i, :, :].rearrange("p j e -> p e j"),
+                    start=True,
+                    stop=True,
+                )
+
+        def copy_v(chunk, pair):
+            if chunk not in v_grouped:
+                v_grouped[chunk] = work.tile([P, H, DH, PACK], BF16, name="v_grouped", align_bytes=64)
+            heads = slice(pair * PAIR, (pair + 1) * PAIR)
+            nc.scalar.copy(
+                out=v_grouped[chunk][:, heads, :, :].rearrange("p h e j -> p (h e j)"),
+                in_=v_ps[chunk, pair][:].rearrange("p i n -> p (i n)"),
             )
 
         def quantise_v(chunk):
@@ -165,19 +185,28 @@ def tile_mhla2_pa_t_e_kernel(tc, x_k, W_K_words, W_K_scales, v_heads, out):
             )
 
         def invert_sums(s, first, last):
-            inv[s, first] = small.tile([P, PACK, last - first], F32, name="inv%d" % first)
-            nc.vector.reciprocal(out=inv[s, first][:], in_=sums[s][:, :, first:last])
+            inverses = small.tile([P, PACK, last - first], F32, name="inv%d" % (last - first))
+            nc.vector.reciprocal(out=inverses[:], in_=sums[s][:, :, first:last])
+            for h in range(first, last):
+                inv[s, h] = inverses[:, :, h - first]
 
-        def scale_p(s, h, engine, first):
+        def scale_p(s, h, engine, first=0, last=DH):
             if s not in p_grouped:
                 p_grouped[s] = work.tile([P, HALF, DH, PACK], BF16, name="p_grouped", align_bytes=64)
-            inv_of_token = inv[s, first][:, :, h - first].unsqueeze(1).unsqueeze(3)
             engine.tensor_tensor(
-                out=p_grouped[s][:, h, :, :].rearrange("p (c i) j -> p c j i", i=RUN),
-                in0=expo[s][:, :, h, :].rearrange("p j (c i) -> p c j i", i=RUN),
-                in1=inv_of_token.to_broadcast([P, DH // RUN, PACK, RUN]),
+                out=p_grouped[s][:, h, first:last, :].rearrange("p (c i) j -> p c j i", i=RUN),
+                in0=expo[s][:, :, h, first:last].rearrange("p j (c i) -> p c j i", i=RUN),
+                in1=inv[s, h].unsqueeze(1).unsqueeze(3).to_broadcast([P, (last - first) // RUN, PACK, RUN]),
                 op=ALU.mult,
             )
+
+        def scale_p_on_scalar(s, h):
+            if s not in p_grouped:
+                p_grouped[s] = work.tile([P, HALF, DH, PACK], BF16, name="p_grouped", align_bytes=64)
+            for j in range(PACK):
+                nc.scalar.activation(
+                    out=p_grouped[s][:, h, :, j], in_=expo[s][:, j, h, :], func=ACT.Copy, scale=inv[s, h][:, j : j + 1]
+                )
 
         def quantise_p(s, first, last):
             chunk, hh = divmod(s, HALVES)
@@ -206,12 +235,17 @@ def tile_mhla2_pa_t_e_kernel(tc, x_k, W_K_words, W_K_scales, v_heads, out):
                         start=(g == 0),
                         stop=(g == CHUNKS_PER_BATCH - 1),
                     )
+            o_banks[b, first] = o_ps
+
+        def store(b, first, last):
             o_sb = work.tile([P, last - first, DH], F32, name="o_sb%d" % (last - first), bufs=HALF)
-            nc.scalar.copy(out=o_sb[:], in_=o_ps[:])
+            nc.scalar.copy(out=o_sb[:], in_=o_banks[b, first][:])
             nc.sync.dma_start(out=out[b, first:last, :, :].rearrange("h d e -> d h e"), in_=o_sb[:])
 
         ident = const.tile([P, P], F32)
         make_identity(nc, ident[:])
+        ident_bf16 = const.tile([P, P], BF16)
+        nc.vector.tensor_copy(out=ident_bf16[:], in_=ident[:])
         w_codes = const.tile([P, F_PASSES, H, PACK * DH], U8, align_bytes=64)
         w_scales = const.tile([P, F_PASSES, H, DH], U8, align_bytes=64)
         w_scales_as_loaded = const.tile([P, H, F_PASSES, DH], U8)
@@ -231,100 +265,167 @@ def tile_mhla2_pa_t_e_kernel(tc, x_k, W_K_words, W_K_scales, v_heads, out):
                     out=w_codes[:, c, heads, :].bitcast(I32), in_=code_words[c][:, heads, :]
                 )
 
-        for j in range(PACK):
-            load_x(0, j)
-        load_w_codes(0)
         scale_rows = W_K_scales.bitcast(I32).rearrange("(h c) (q r) w -> q r h c w", c=F_PASSES, r=4)
-        for q in range(4):
-            nc.sync.dma_start(
-                out=w_scales_as_loaded[32 * q : 32 * q + 4, :, :, :].bitcast(I32), in_=scale_rows[q]
+
+        def load_w_scales():
+            for q in range(4):
+                nc.sync.dma_start(
+                    out=w_scales_as_loaded[32 * q : 32 * q + 4, :, :, :].bitcast(I32), in_=scale_rows[q]
+                )
+
+        def move_w_scales():
+            nc.vector.tensor_copy(
+                out=w_scales[:].bitcast(I32),
+                in_=w_scales_as_loaded[:].bitcast(I32).rearrange("p h c w -> p c h w"),
             )
-        for pair in range(PACK):
-            load_v(0, pair)
+
+        load_x(0, 0)
+        load_x(0, 1)
+        load_w_codes(0)
+        load_w_scales()
+        load_x(0, 2)
+        load_x(0, 3)
         load_w_codes(1)
-        for chunk in range(1, LOAD_AHEAD):
-            for j in range(PACK):
-                load_x(chunk, j)
+        load_x(1, 0)
+        load_x(1, 1)
+        load_v(0, 0)
+        load_v(0, 1)
+        load_x(1, 2)
+        load_x(1, 3)
+        load_v(0, 2)
+        load_v(0, 3)
+        for j in range(PACK):
+            load_x(2, j)
+        for chunk in (1, 2):
             for pair in range(PACK):
                 load_v(chunk, pair)
-
+        transpose_x(0, 0)
+        copy_x(0, 0)
+        quantise_x(0, 0)
+        transpose_x(0, 1)
+        copy_x(0, 1)
+        move_w_scales()
+        project(0)
+        quantise_x(0, 1)
+        transpose_x(0, 2)
+        copy_x(0, 2)
+        find_top(0)
+        make_shifts(0, (0,))
+        project(1)
+        quantise_x(0, 2)
+        transpose_x(0, 3)
+        copy_x(0, 3)
+        find_top(1)
+        make_shifts(0, (1,))
+        project(2)
+        quantise_x(0, 3)
+        project(3)
+        project(4)
+        find_top(2)
+        find_top(3)
+        regroup_v(0, 0, nc.vector.tensor_copy)
+        regroup_v(0, 1, nc.vector.tensor_copy)
+        for j in range(PACK):
+            load_x(LOAD_AHEAD, j)
         last = GROUPS - 1
-        for t in range(-BANKS_PER_CHUNK, BANKS + PACK):
+        for t in range(BANKS + 1):
             group, phase = divmod(t, PACK)
             chunk, hh = divmod(group, HALVES)
             following = chunk + 1
             step = t % BANKS_PER_CHUNK
-
-            if hh == 0 and following < CHUNKS:
-                transpose_x(following, phase)
-            if 0 <= t + TENSOR_LEAD < BANKS:
+            done = group - 1
+            scaling = 0 <= done < last
+            ts = t + 0
+            if ts % 8 < 4 and ts // 8 + 1 < CHUNKS:
+                if t == 0:
+                    for q in range(0):
+                        transpose_x(1, q)
+                transpose_x(ts // 8 + 1, ts % 8)
+            if step - 4 in {1: 2, 3: 3} and following < CHUNKS:
+                multiply_v(following, {1: 2, 3: 3}[step - 4])
+            if 5 <= t + TENSOR_LEAD < BANKS:
                 project(t + TENSOR_LEAD)
-
-            if 0 <= group - 1 < last:
+            if scaling and phase in (1, 3):
+                unit = 2 if phase == 1 else 3
                 if phase == 1:
-                    invert_sums(group - 1, 0, 3)
-                    scale_p(group - 1, 2, nc.gpsimd if group < last else nc.vector, 0)
-                if phase == 3:
-                    invert_sums(group - 1, 3, 4)
-                    scale_p(group - 1, 3, nc.gpsimd if group < last else nc.vector, 3)
+                    invert_sums(done, 0, 3)
+                else:
+                    invert_sums(done, 3, 4)
+                if group < last:
+                    scale_p(done, unit, nc.gpsimd, 0, GC)
+                else:
+                    scale_p(done, unit, nc.vector)
             if phase % 2 == 1:
                 for bank in (t + VECTOR_LEAD, t + VECTOR_LEAD + 1):
-                    if 0 <= bank < BANKS:
+                    if 4 <= bank < BANKS:
                         find_top(bank)
-            if 0 <= group - 1 < last and phase in (1, 2):
-                scale_p(group - 1, phase - 1, nc.vector, 0)
-            if phase == 1 and 0 <= group - 2 < last - 1:
+            if scaling and phase == 1:
+                scale_p(done, 0, nc.vector)
+            if scaling and phase == 2:
+                scale_p(done, 1, nc.vector)
+            if scaling and phase in (1, 3) and GC < DH and group < last:
+                scale_p(done, unit, nc.vector, GC, DH)
+            if phase == 0 and 0 <= group - 2 < last - 1:
                 quantise_p(group - 2, 0, HALF)
-            if step == 4 and 0 <= chunk < CHUNKS:
-                quantise_v(chunk)
             for head in FIRST_V.get(t, ()):
-                regroup_v(0, head)
-            if step in (2, 4, 6) and 0 < following < CHUNKS:
-                regroup_v(following, step // 2 - 1)
-
-            if 0 <= group < last:
+                regroup_v(0, head, nc.vector.tensor_copy)
+            if step in (4,) and following < CHUNKS:
+                regroup_v(following, (4,).index(step), nc.vector.tensor_copy)
+            if step == 7 and 0 <= chunk < 7:
+                quantise_v(chunk)
+            if group < last:
                 for h in range(HALF):
                     exponentials(group, phase, h)
             if group == last:
                 for j in range(PACK):
                     exponentials(group, j, phase)
-            if t == -1:
-                make_shifts(0, (0,))
-                make_shifts(0, (1,))
-            elif phase % 2 == 1 and 0 <= t + 1 and group < last:
+            if phase % 2 == 1 and group < last:
                 make_shifts((t + 1) // 2, (0, 1))
-                if group == last - 1 and phase == 3:
+                if t == BANKS - PACK - 1:
                     make_shifts((t + 3) // 2, (0, 1))
             if hh == 0 and following < CHUNKS:
                 copy_x(following, phase)
-            if hh == 1 and 0 < following < CHUNKS:
-                regroup_v(following, V_HEADS + phase)
-                if phase == PACK - 1:
-                    regroup_v(following, H - 1)
-            if 1 <= step <= PACK and following < CHUNKS:
-                quantise_x(following, step - 1)
-            if t == 1 - BANKS_PER_CHUNK:
-                nc.vector.tensor_copy(
-                    out=w_scales[:].bitcast(I32),
-                    in_=w_scales_as_loaded[:].bitcast(I32).rearrange("p h c w -> p c h w"),
-                )
-
+            if hh == 1 and following < CHUNKS:
+                for head in {0: [], 1: [1], 2: [2], 3: [3]}[phase]:
+                    regroup_v(following, head, nc.scalar.copy)
+                if phase - 0 in {1: 2, 3: 3}:
+                    copy_v(following, {1: 2, 3: 3}[phase - 0])
+            if following < CHUNKS:
+                for j in QX.get(step, ()):
+                    quantise_x(following, j)
             if phase == PACK - 1 and hh == 0 and following + LOAD_AHEAD < CHUNKS:
                 for j in range(PACK):
                     load_x(following + LOAD_AHEAD, j)
-            if phase == PACK - 1 and hh == 0 and 0 <= chunk < CHUNKS - LOAD_AHEAD:
+            if step == 7 and 0 <= chunk < CHUNKS - LOAD_AHEAD:
                 for pair in range(PACK):
                     load_v(chunk + LOAD_AHEAD, pair)
-
-            if phase == 2 and 0 <= group - 2 < last - 1:
-                summed_chunk, summed_hh = divmod(group - 2, HALVES)
-                if (summed_chunk + 1) % CHUNKS_PER_BATCH == 0:
-                    summarise(summed_chunk // CHUNKS_PER_BATCH, summed_hh * HALF, (summed_hh + 1) * HALF)
-            if group == last + 1:
-                if phase == 0:
-                    quantise_p(last - 1, 0, HALF)
-                    summarise(B - 1, 0, HALF)
-                invert_sums(last, phase, phase + 1)
-                scale_p(last, phase, nc.vector, phase)
-                quantise_p(last, phase, phase + 1)
-                summarise(B - 1, HALF + phase, HALF + phase + 1)
+            for i in range(B * HALVES // 2):
+                if t == (57, 61)[i]:
+                    summarise(0, i * HALF, (i + 1) * HALF)
+                if t == (57, 61)[i] + 1:
+                    store(0, i * HALF, (i + 1) * HALF)
+            if t == BANKS:
+                invert_sums(last, 0, 1)
+                quantise_v(CHUNKS - 1)
+                scale_p(last, 0, nc.vector)
+                invert_sums(last, 1, 2)
+                quantise_p(last - 1, 0, HALF)
+                summarise(B - 1, 0, HALF)
+                scale_p(last, 1, nc.vector)
+                quantise_p(last, 0, 1)
+                summarise(B - 1, HALF + 0, HALF + 1)
+                store(B - 1, 0, HALF)
+                invert_sums(last, 2, 3)
+                scale_p(last, 2, nc.vector)
+                quantise_p(last, 1, 2)
+                summarise(B - 1, HALF + 1, HALF + 2)
+                store(B - 1, HALF + 0, HALF + 1)
+                invert_sums(last, 3, 4)
+                scale_p(last, 3, nc.vector)
+                quantise_p(last, 2, 3)
+                summarise(B - 1, HALF + 2, HALF + 3)
+                store(B - 1, HALF + 1, HALF + 2)
+                quantise_p(last, 3, 4)
+                summarise(B - 1, HALF + 3, HALF + 4)
+                store(B - 1, HALF + 2, HALF + 3)
+                store(B - 1, HALF + 3, HALF + 4)

@@ -285,13 +285,13 @@ def tile_mhla2_pa_t_e_kernel(tc, x_k, W_K_words, W_K_scales, v_heads, out):
         load_w_scales()
         load_x(0, 2)
         load_x(0, 3)
+        load_v(0, 0)
         load_w_codes(1)
         load_x(1, 0)
         load_x(1, 1)
-        load_v(0, 0)
-        load_v(0, 1)
         load_x(1, 2)
         load_x(1, 3)
+        load_v(0, 1)
         load_v(0, 2)
         load_v(0, 3)
         for j in range(PACK):
@@ -334,13 +334,12 @@ def tile_mhla2_pa_t_e_kernel(tc, x_k, W_K_words, W_K_scales, v_heads, out):
             following = chunk + 1
             step = t % BANKS_PER_CHUNK
             done = group - 1
-            scaling = 0 <= done < last
-            ts = t + 0
-            if ts % 8 < 4 and ts // 8 + 1 < CHUNKS:
-                if t == 0:
-                    for q in range(0):
-                        transpose_x(1, q)
-                transpose_x(ts // 8 + 1, ts % 8)
+            scaling = 0 <= done < last - 1
+            if group == last and phase == 0:
+                invert_sums(last - 1, 0, HALF)
+            if following < CHUNKS:
+                for j in {0: (0,), 1: (1,), 2: (2,), 3: (3,)}.get(step, ()):
+                    transpose_x(following, j)
             if step - 4 in {1: 2, 3: 3} and following < CHUNKS:
                 multiply_v(following, {1: 2, 3: 3}[step - 4])
             if 5 <= t + TENSOR_LEAD < BANKS:
@@ -351,10 +350,11 @@ def tile_mhla2_pa_t_e_kernel(tc, x_k, W_K_words, W_K_scales, v_heads, out):
                     invert_sums(done, 0, 3)
                 else:
                     invert_sums(done, 3, 4)
-                if group < last:
-                    scale_p(done, unit, nc.gpsimd, 0, GC)
-                else:
-                    scale_p(done, unit, nc.vector)
+                scale_p(done, unit, nc.gpsimd, 0, GC)
+            if phase in {1: (2, 3, 0), 3: (1, 2, 0)}:
+                d, unit_, cond = {1: (2, 3, 0), 3: (1, 2, 0)}[phase]
+                if 0 <= group - d < last - 1:
+                    scale_p(group - d, unit_, nc.vector, GC, DH)
             if phase % 2 == 1:
                 for bank in (t + VECTOR_LEAD, t + VECTOR_LEAD + 1):
                     if 4 <= bank < BANKS:
@@ -363,10 +363,13 @@ def tile_mhla2_pa_t_e_kernel(tc, x_k, W_K_words, W_K_scales, v_heads, out):
                 scale_p(done, 0, nc.vector)
             if scaling and phase == 2:
                 scale_p(done, 1, nc.vector)
-            if scaling and phase in (1, 3) and GC < DH and group < last:
+            if not {1: (2, 3, 0), 3: (1, 2, 0)} and scaling and phase in (1, 3) and GC < DH:
                 scale_p(done, unit, nc.vector, GC, DH)
-            if phase == 0 and 0 <= group - 2 < last - 1:
+            if phase == 2 and 0 <= group - 2 < last - 1:
                 quantise_p(group - 2, 0, HALF)
+            if group == last and phase == 0:
+                for h in range(HALF):
+                    scale_p(last - 1, h, nc.vector)
             for head in FIRST_V.get(t, ()):
                 regroup_v(0, head, nc.vector.tensor_copy)
             if step in (4,) and following < CHUNKS:
@@ -405,27 +408,27 @@ def tile_mhla2_pa_t_e_kernel(tc, x_k, W_K_words, W_K_scales, v_heads, out):
                 if t == (57, 61)[i] + 1:
                     store(0, i * HALF, (i + 1) * HALF)
             if t == BANKS:
-                invert_sums(last, 0, 1)
                 quantise_v(CHUNKS - 1)
+                invert_sums(last, 3, 4)
+                invert_sums(last, 0, 1)
+                quantise_p(last - 1, 0, HALF)
+                scale_p_on_scalar(last, 3)
+                summarise(B - 1, 0, HALF)
                 scale_p(last, 0, nc.vector)
                 invert_sums(last, 1, 2)
-                quantise_p(last - 1, 0, HALF)
-                summarise(B - 1, 0, HALF)
                 scale_p(last, 1, nc.vector)
                 quantise_p(last, 0, 1)
                 summarise(B - 1, HALF + 0, HALF + 1)
-                store(B - 1, 0, HALF)
                 invert_sums(last, 2, 3)
                 scale_p(last, 2, nc.vector)
+                store(B - 1, 0, HALF)
                 quantise_p(last, 1, 2)
                 summarise(B - 1, HALF + 1, HALF + 2)
                 store(B - 1, HALF + 0, HALF + 1)
-                invert_sums(last, 3, 4)
-                scale_p(last, 3, nc.vector)
-                quantise_p(last, 2, 3)
-                summarise(B - 1, HALF + 2, HALF + 3)
-                store(B - 1, HALF + 1, HALF + 2)
                 quantise_p(last, 3, 4)
                 summarise(B - 1, HALF + 3, HALF + 4)
-                store(B - 1, HALF + 2, HALF + 3)
+                store(B - 1, HALF + 1, HALF + 2)
+                quantise_p(last, 2, 3)
+                summarise(B - 1, HALF + 2, HALF + 3)
                 store(B - 1, HALF + 3, HALF + 4)
+                store(B - 1, HALF + 2, HALF + 3)

@@ -110,24 +110,23 @@ def tile_mhla2_pa_t_e_kernel(tc, x_k, W_K_words, W_K_scales, v_heads, out):
                 in_=v_sb[chunk][:, head, :, :].rearrange("p j (c i) -> p c j i", i=RUN),
             )
 
-        def multiply_v(chunk, pair):
-            v_ps[chunk, pair] = psum_t.tile([P, PAIR, DH * PACK], BF16, name="x_ps")
-            for i in range(PAIR):
+        def multiply_v(chunk, first, last):
+            v_ps[chunk, first] = psum_t.tile([P, last - first, DH * PACK], BF16, name="x_ps")
+            for head in range(first, last):
                 nc.tensor.matmul(
-                    v_ps[chunk, pair][:, i, :],
+                    v_ps[chunk, first][:, head - first, :],
                     lhsT=ident_bf16[:],
-                    rhs=v_sb[chunk][:, pair * PAIR + i, :, :].rearrange("p j e -> p e j"),
+                    rhs=v_sb[chunk][:, head, :, :].rearrange("p j e -> p e j"),
                     start=True,
                     stop=True,
                 )
 
-        def copy_v(chunk, pair):
+        def copy_v(chunk, first, last):
             if chunk not in v_grouped:
                 v_grouped[chunk] = work.tile([P, H, DH, PACK], BF16, name="v_grouped", align_bytes=64)
-            heads = slice(pair * PAIR, (pair + 1) * PAIR)
             nc.scalar.copy(
-                out=v_grouped[chunk][:, heads, :, :].rearrange("p h e j -> p (h e j)"),
-                in_=v_ps[chunk, pair][:].rearrange("p i n -> p (i n)"),
+                out=v_grouped[chunk][:, first:last, :, :].rearrange("p h e j -> p (h e j)"),
+                in_=v_ps[chunk, first][:].rearrange("p i n -> p (i n)"),
             )
 
         def quantise_v(chunk):
@@ -281,14 +280,14 @@ def tile_mhla2_pa_t_e_kernel(tc, x_k, W_K_words, W_K_scales, v_heads, out):
 
         load_x(0, 0)
         load_x(0, 1)
-        load_w_codes(0)
         load_w_scales()
         load_x(0, 2)
+        load_w_codes(0)
         load_x(0, 3)
-        load_v(0, 0)
         load_w_codes(1)
         load_x(1, 0)
         load_x(1, 1)
+        load_v(0, 0)
         load_x(1, 2)
         load_x(1, 3)
         load_v(0, 1)
@@ -304,21 +303,21 @@ def tile_mhla2_pa_t_e_kernel(tc, x_k, W_K_words, W_K_scales, v_heads, out):
         quantise_x(0, 0)
         transpose_x(0, 1)
         copy_x(0, 1)
-        move_w_scales()
-        project(0)
         quantise_x(0, 1)
         transpose_x(0, 2)
         copy_x(0, 2)
-        find_top(0)
-        make_shifts(0, (0,))
-        project(1)
+        move_w_scales()
+        project(0)
         quantise_x(0, 2)
         transpose_x(0, 3)
         copy_x(0, 3)
+        find_top(0)
+        make_shifts(0, (0,))
+        quantise_x(0, 3)
+        project(1)
         find_top(1)
         make_shifts(0, (1,))
         project(2)
-        quantise_x(0, 3)
         project(3)
         project(4)
         find_top(2)
@@ -338,10 +337,11 @@ def tile_mhla2_pa_t_e_kernel(tc, x_k, W_K_words, W_K_scales, v_heads, out):
             if group == last and phase == 0:
                 invert_sums(last - 1, 0, HALF)
             if following < CHUNKS:
-                for j in {0: (0,), 1: (1,), 2: (2,), 3: (3,)}.get(step, ()):
-                    transpose_x(following, j)
-            if step - 4 in {1: 2, 3: 3} and following < CHUNKS:
-                multiply_v(following, {1: 2, 3: 3}[step - 4])
+                for j in {0: (0,), 1: (1, 2), 3: (3,)}.get(step, ()):
+                    if t >= PACK or j >= 0:
+                        transpose_x(following, j)
+            if step - 4 in {1: (4, 6), 3: (6, 8)} and following < CHUNKS:
+                multiply_v(following, *{1: (4, 6), 3: (6, 8)}[step - 4])
             if 5 <= t + TENSOR_LEAD < BANKS:
                 project(t + TENSOR_LEAD)
             if scaling and phase in (1, 3):
@@ -361,7 +361,7 @@ def tile_mhla2_pa_t_e_kernel(tc, x_k, W_K_words, W_K_scales, v_heads, out):
                         find_top(bank)
             if scaling and phase == 1:
                 scale_p(done, 0, nc.vector)
-            if scaling and phase == 2:
+            if scaling and phase == 2 and (done, 1) not in {}.values():
                 scale_p(done, 1, nc.vector)
             if not {1: (2, 3, 0), 3: (1, 2, 0)} and scaling and phase in (1, 3) and GC < DH:
                 scale_p(done, unit, nc.vector, GC, DH)
@@ -369,19 +369,22 @@ def tile_mhla2_pa_t_e_kernel(tc, x_k, W_K_words, W_K_scales, v_heads, out):
                 quantise_p(group - 2, 0, HALF)
             if group == last and phase == 0:
                 for h in range(HALF):
-                    scale_p(last - 1, h, nc.vector)
+                    if (last - 1, h) not in {}.values():
+                        scale_p(last - 1, h, nc.vector)
             for head in FIRST_V.get(t, ()):
                 regroup_v(0, head, nc.vector.tensor_copy)
             if step in (4,) and following < CHUNKS:
                 regroup_v(following, (4,).index(step), nc.vector.tensor_copy)
             if step == 7 and 0 <= chunk < 7:
                 quantise_v(chunk)
-            if group < last:
+            if group < last and t >= 0:
                 for h in range(HALF):
                     exponentials(group, phase, h)
             if group == last:
                 for j in range(PACK):
                     exponentials(group, j, phase)
+            if t in {}:
+                scale_p_on_scalar({}[t][0], {}[t][1])
             if phase % 2 == 1 and group < last:
                 make_shifts((t + 1) // 2, (0, 1))
                 if t == BANKS - PACK - 1:
@@ -391,8 +394,8 @@ def tile_mhla2_pa_t_e_kernel(tc, x_k, W_K_words, W_K_scales, v_heads, out):
             if hh == 1 and following < CHUNKS:
                 for head in {0: [], 1: [1], 2: [2], 3: [3]}[phase]:
                     regroup_v(following, head, nc.scalar.copy)
-                if phase - 0 in {1: 2, 3: 3}:
-                    copy_v(following, {1: 2, 3: 3}[phase - 0])
+                if phase - 0 in {1: (4, 6), 3: (6, 8)}:
+                    copy_v(following, *{1: (4, 6), 3: (6, 8)}[phase - 0])
             if following < CHUNKS:
                 for j in QX.get(step, ()):
                     quantise_x(following, j)
@@ -403,23 +406,23 @@ def tile_mhla2_pa_t_e_kernel(tc, x_k, W_K_words, W_K_scales, v_heads, out):
                 for pair in range(PACK):
                     load_v(chunk + LOAD_AHEAD, pair)
             for i in range(B * HALVES // 2):
-                if t == (57, 61)[i]:
+                if t == (57, 59)[i]:
                     summarise(0, i * HALF, (i + 1) * HALF)
-                if t == (57, 61)[i] + 1:
+                if t == (57, 59)[i] + 1:
                     store(0, i * HALF, (i + 1) * HALF)
             if t == BANKS:
                 quantise_v(CHUNKS - 1)
                 invert_sums(last, 3, 4)
+                invert_sums(last, 2, 3)
                 invert_sums(last, 0, 1)
-                quantise_p(last - 1, 0, HALF)
                 scale_p_on_scalar(last, 3)
+                quantise_p(last - 1, 0, HALF)
                 summarise(B - 1, 0, HALF)
                 scale_p(last, 0, nc.vector)
                 invert_sums(last, 1, 2)
                 scale_p(last, 1, nc.vector)
                 quantise_p(last, 0, 1)
                 summarise(B - 1, HALF + 0, HALF + 1)
-                invert_sums(last, 2, 3)
                 scale_p(last, 2, nc.vector)
                 store(B - 1, 0, HALF)
                 quantise_p(last, 1, 2)

from contextlib import ExitStack

import concourse.mybir as mybir
from concourse.masks import make_identity

F32 = mybir.dt.float32
BF16 = mybir.dt.bfloat16
I32 = mybir.dt.int32
U32 = mybir.dt.uint32
U8 = mybir.dt.uint8
FP8X4 = mybir.dt.float8_e4m3fn_x4
ALU = mybir.AluOpType
ACT = mybir.ActivationFunctionType
AXIS = mybir.AxisListType

B, S, D, H, DH = 2, 2048, 1024, 8, 128
P = 128
PACK = 4
K_PASS = P * PACK
F_PASSES = D // K_PASS
CHUNKS_PER_BATCH = S // K_PASS
CHUNKS = B * CHUNKS_PER_BATCH
HALF = 4
HALVES = H // HALF
BANKS_PER_CHUNK = HALVES * PACK
BANKS = CHUNKS * BANKS_PER_CHUNK
PAIR = H // PACK
SOFTMAX_SCALE = 128.0 ** -0.25
LOAD_AHEAD = 3
TENSOR_LEAD = 5
VECTOR_LEAD = 3
GROUPS = CHUNKS * HALVES
FIRST_V = {2: (2, 3, 4), 4: (5, 6, 7)}
GC=96
QX={1: (0,), 2: (1,), 3: (2,), 4: (3,)}
RUN = 8

FLOPS = 2 * B * S * D * H * DH + 2 * B * H * S * DH * DH


def tile_mhla2_pa_t_e_kernel(tc, x_k, W_K_words, W_K_scales, v_heads, out):
    nc = tc.nc
    with ExitStack() as ctx:
        ctx.enter_context(tc.manual_schedule())
        const = ctx.enter_context(tc.tile_pool(name="const", bufs=1))
        loads = ctx.enter_context(tc.tile_pool(name="loads", bufs=LOAD_AHEAD))
        work = ctx.enter_context(tc.tile_pool(name="work", bufs=2))
        small = ctx.enter_context(tc.tile_pool(name="small", bufs=8))
        keep = ctx.enter_context(tc.tile_pool(name="keep", bufs=B))
        psum_t = ctx.enter_context(tc.psum_pool(name="psum_t", bufs=2))
        psum_k = ctx.enter_context(tc.psum_pool(name="psum_k", bufs=6))

        x_sb, x_ps, x_grouped, x_codes, x_scales = {}, {}, {}, {}, {}
        v_sb, v_ps, v_grouped, v_codes, v_scales = {}, {}, {}, {}, {}
        k_ps, top, shift, expo, sums, inv = {}, {}, {}, {}, {}, {}
        p_grouped, p_codes, p_scales, o_banks = {}, {}, {}, {}

        def load_x(chunk, j):
            if j == 0:
                x_sb[chunk] = loads.tile([P, PACK, D], BF16, name="x_sb")
            b, g = divmod(chunk, CHUNKS_PER_BATCH)
            rows = x_k[b, g * K_PASS : (g + 1) * K_PASS, :].rearrange("(p j) f -> p j f", j=PACK)
            nc.sync.dma_start(out=x_sb[chunk][:, j, :], in_=rows[:, j, :])

        def load_v(chunk, pair):
            if pair == 0:
                v_sb[chunk] = loads.tile([P, H, PACK, DH], BF16, name="v_sb")
            b, g = divmod(chunk, CHUNKS_PER_BATCH)
            heads = slice(pair * PAIR, (pair + 1) * PAIR)
            rows = v_heads[b, heads, g * K_PASS : (g + 1) * K_PASS, :]
            nc.sync.dma_start(
                out=v_sb[chunk][:, heads, :, :], in_=rows.rearrange("h (p j) e -> p h j e", j=PACK)
            )

        def transpose_x(chunk, j):
            x_words = x_sb[chunk][:].bitcast(F32)
            x_ps[chunk, j] = psum_t.tile([P, F_PASSES, 2, P], F32, name="x_ps")
            for c in range(F_PASSES):
                for u in range(2):
                    nc.tensor.transpose(
                        x_ps[chunk, j][:, c, u, :],
                        x_words[:, j, 256 * c + u : 256 * (c + 1) : 2],
                        ident[:],
                    )

        def copy_x(chunk, j):
            x_grouped[chunk, j] = work.tile(
                [P, F_PASSES, P, PACK], BF16, name="x_grouped", bufs=3, align_bytes=64
            )
            nc.scalar.copy(
                out=x_grouped[chunk, j][:].bitcast(F32),
                in_=x_ps[chunk, j][:].rearrange("q c u t -> q c t u"),
            )

        def quantise_x(chunk, j):
            if j == 0:
                x_codes[chunk] = work.tile([P, PACK, F_PASSES, P], U32, name="x_codes", align_bytes=64)
                x_scales[chunk] = work.tile([P, PACK, F_PASSES, P], U8, name="x_scales", align_bytes=64)
            nc.vector.quantize_mx(
                out=x_codes[chunk][:, j, :, :].rearrange("q c t -> q (c t)").bitcast(FP8X4),
                scales=x_scales[chunk][:, j, :, :].rearrange("q c t -> q (c t)"),
                in_=x_grouped[chunk, j][:].rearrange("q c t w -> q (c t w)"),
            )

        def regroup_v(chunk, head, copy):
            if chunk not in v_grouped:
                v_grouped[chunk] = work.tile([P, H, DH, PACK], BF16, name="v_grouped", align_bytes=64)
            copy(
                out=v_grouped[chunk][:, head, :, :].rearrange("p (c i) j -> p c j i", i=RUN),
                in_=v_sb[chunk][:, head, :, :].rearrange("p j (c i) -> p c j i", i=RUN),
            )

        def multiply_v(chunk, first, last):
            v_ps[chunk, first] = psum_t.tile([P, last - first, DH * PACK], BF16, name="x_ps")
            for head in range(first, last):
                nc.tensor.matmul(
                    v_ps[chunk, first][:, head - first, :],
                    lhsT=ident_bf16[:],
                    rhs=v_sb[chunk][:, head, :, :].rearrange("p j e -> p e j"),
                    start=True,
                    stop=True,
                )

        def copy_v(chunk, first, last):
            if chunk not in v_grouped:
                v_grouped[chunk] = work.tile([P, H, DH, PACK], BF16, name="v_grouped", align_bytes=64)
            nc.scalar.copy(
                out=v_grouped[chunk][:, first:last, :, :].rearrange("p h e j -> p (h e j)"),
                in_=v_ps[chunk, first][:].rearrange("p i n -> p (i n)"),
            )

        def quantise_v(chunk):
            b, g = divmod(chunk, CHUNKS_PER_BATCH)
            if g == 0:
                v_codes[b] = keep.tile([P, CHUNKS_PER_BATCH, H, DH], U32, name="v_codes", align_bytes=64)
                v_scales[b] = keep.tile([P, CHUNKS_PER_BATCH, H, DH], U8, name="v_scales", align_bytes=64)
            nc.vector.quantize_mx(
                out=v_codes[b][:, g, :, :].rearrange("p h e -> p (h e)").bitcast(FP8X4),
                scales=v_scales[b][:, g, :, :].rearrange("p h e -> p (h e)"),
                in_=v_grouped[chunk][:].rearrange("p h e j -> p (h e j)"),
            )

        def project(t):
            chunk, n = divmod(t, BANKS_PER_CHUNK)
            hh, j = divmod(n, PACK)
            heads = slice(hh * HALF, (hh + 1) * HALF)
            k_ps[t] = psum_k.tile([P, HALF, DH], F32, name="k_ps")
            for c in range(F_PASSES):
                nc.tensor.matmul_mx(
                    out=k_ps[t][:].rearrange("p h d -> p (h d)"),
                    lhsT=x_codes[chunk][:, j, c, :].bitcast(FP8X4),
                    lhsT_scale=x_scales[chunk][:, j, c, :],
                    rhs=w_codes[:, c, heads, :].rearrange("p h n -> p (h n)").bitcast(FP8X4),
                    rhs_scale=w_scales[:, c, heads, :].rearrange("p h n -> p (h n)"),
                    start=(c == 0),
                    stop=(c == F_PASSES - 1),
                )

        def find_top(t):
            if t % 2 == 0:
                top[t // 2] = small.tile([P, 2, HALF], F32, name="top")
            nc.vector.tensor_reduce(out=top[t // 2][:, t % 2, :], in_=k_ps[t][:], axis=AXIS.X, op=ALU.max)

        def make_shifts(u, banks):
            shifts = small.tile([P, len(banks), HALF], F32, name="shift%d" % len(banks))
            nc.scalar.mul(
                out=shifts[:], in_=top[u][:, banks[0] : banks[-1] + 1, :], mul=-SOFTMAX_SCALE
            )
            for i, bank in enumerate(banks):
                shift[2 * u + bank] = shifts[:, i, :]

        def exponentials(s, j, h):
            if j == 0 and h == 0:
                expo[s] = work.tile([P, PACK, HALF, DH], F32, name="expo", bufs=3)
                sums[s] = small.tile([P, PACK, HALF], F32, name="sums")
            t = s * PACK + j
            nc.scalar.activation(
                out=expo[s][:, j, h, :],
                in_=k_ps[t][:, h, :],
                func=ACT.Exp,
                bias=shift[t][:, h : h + 1],
                scale=SOFTMAX_SCALE,
                accum_out=sums[s][:, j, h : h + 1],
            )

        def invert_sums(s, first, last):
            inverses = small.tile([P, PACK, last - first], F32, name="inv%d" % (last - first))
            nc.vector.reciprocal(out=inverses[:], in_=sums[s][:, :, first:last])
            for h in range(first, last):
                inv[s, h] = inverses[:, :, h - first]

        def scale_p(s, h, engine, first=0, last=DH):
            if s not in p_grouped:
                p_grouped[s] = work.tile([P, HALF, DH, PACK], BF16, name="p_grouped", align_bytes=64)
            engine.tensor_tensor(
                out=p_grouped[s][:, h, first:last, :].rearrange("p (c i) j -> p c j i", i=RUN),
                in0=expo[s][:, :, h, first:last].rearrange("p j (c i) -> p c j i", i=RUN),
                in1=inv[s, h].unsqueeze(1).unsqueeze(3).to_broadcast([P, (last - first) // RUN, PACK, RUN]),
                op=ALU.mult,
            )

        def scale_p_on_scalar(s, h):
            if s not in p_grouped:
                p_grouped[s] = work.tile([P, HALF, DH, PACK], BF16, name="p_grouped", align_bytes=64)
            for j in range(PACK):
                nc.scalar.activation(
                    out=p_grouped[s][:, h, :, j], in_=expo[s][:, j, h, :], func=ACT.Copy, scale=inv[s, h][:, j : j + 1]
                )

        def quantise_p(s, first, last):
            chunk, hh = divmod(s, HALVES)
            b, g = divmod(chunk, CHUNKS_PER_BATCH)
            if g == 0 and hh == 0 and first == 0:
                p_codes[b] = keep.tile([P, CHUNKS_PER_BATCH, H, DH], U32, name="p_codes", align_bytes=64)
                p_scales[b] = keep.tile([P, CHUNKS_PER_BATCH, H, DH], U8, name="p_scales", align_bytes=64)
            heads = slice(hh * HALF + first, hh * HALF + last)
            nc.vector.quantize_mx(
                out=p_codes[b][:, g, heads, :].rearrange("p h d -> p (h d)").bitcast(FP8X4),
                scales=p_scales[b][:, g, heads, :].rearrange("p h d -> p (h d)"),
                in_=p_grouped[s][:, first:last, :, :].rearrange("p h d j -> p (h d j)"),
            )

        def summarise(b, first, last):
            o_ps = psum_k.tile([P, last - first, DH], F32, name="k_ps")
            for h in range(last - first):
                head = first + h
                for g in range(CHUNKS_PER_BATCH):
                    nc.tensor.matmul_mx(
                        out=o_ps[:, h, :],
                        lhsT=p_codes[b][:, g, head, :].bitcast(FP8X4),
                        lhsT_scale=p_scales[b][:, g, head, :],
                        rhs=v_codes[b][:, g, head, :].bitcast(FP8X4),
                        rhs_scale=v_scales[b][:, g, head, :],
                        start=(g == 0),
                        stop=(g == CHUNKS_PER_BATCH - 1),
                    )
            o_banks[b, first] = o_ps

        def store(b, first, last):
            o_sb = work.tile([P, last - first, DH], F32, name="o_sb%d" % (last - first), bufs=HALF)
            nc.scalar.copy(out=o_sb[:], in_=o_banks[b, first][:])
            nc.sync.dma_start(out=out[b, first:last, :, :].rearrange("h d e -> d h e"), in_=o_sb[:])

        ident = const.tile([P, P], F32)
        make_identity(nc, ident[:])
        ident_bf16 = const.tile([P, P], BF16)
        nc.vector.tensor_copy(out=ident_bf16[:], in_=ident[:])
        w_codes = const.tile([P, F_PASSES, H, PACK * DH], U8, align_bytes=64)
        w_scales = const.tile([P, F_PASSES, H, DH], U8, align_bytes=64)
        w_scales_as_loaded = const.tile([P, H, F_PASSES, DH], U8)
        nc.vector.memset(w_scales_as_loaded[:].rearrange("p h c n -> p (h c n)").bitcast(I32), 0)
        zero = const.tile([P, 1], F32)
        one = const.tile([P, 1], F32)
        nc.vector.memset(zero[:], 0.0)
        nc.scalar.activation(out=one[:], in_=zero[:], func=ACT.Exp)

        code_words = W_K_words.rearrange("g p n t -> g p (n t)").bitcast(I32)
        code_words = code_words.rearrange("(h c) p n -> c p h n", c=F_PASSES)

        def load_w_codes(hh):
            heads = slice(hh * HALF, (hh + 1) * HALF)
            for c in range(F_PASSES):
                nc.sync.dma_start(
                    out=w_codes[:, c, heads, :].bitcast(I32), in_=code_words[c][:, heads, :]
                )

        scale_rows = W_K_scales.bitcast(I32).rearrange("(h c) (q r) w -> q r h c w", c=F_PASSES, r=4)

        def load_w_scales():
            for q in range(4):
                nc.sync.dma_start(
                    out=w_scales_as_loaded[32 * q : 32 * q + 4, :, :, :].bitcast(I32), in_=scale_rows[q]
                )

        def move_w_scales():
            nc.vector.tensor_copy(
                out=w_scales[:].bitcast(I32),
                in_=w_scales_as_loaded[:].bitcast(I32).rearrange("p h c w -> p c h w"),
            )

        load_x(0, 0)
        load_x(0, 1)
        load_w_scales()
        load_x(0, 2)
        load_w_codes(0)
        load_x(0, 3)
        load_w_codes(1)
        load_x(1, 0)
        load_x(1, 1)
        load_v(0, 0)
        load_x(1, 2)
        load_x(1, 3)
        load_v(0, 1)
        load_v(0, 2)
        load_v(0, 3)
        for j in range(PACK):
            load_x(2, j)
        for chunk in (1, 2):
            for pair in range(PACK):
                load_v(chunk, pair)
        transpose_x(0, 0)
        copy_x(0, 0)
        quantise_x(0, 0)
        transpose_x(0, 1)
        copy_x(0, 1)
        quantise_x(0, 1)
        transpose_x(0, 2)
        copy_x(0, 2)
        move_w_scales()
        project(0)
        quantise_x(0, 2)
        transpose_x(0, 3)
        copy_x(0, 3)
        find_top(0)
        make_shifts(0, (0,))
        quantise_x(0, 3)
        project(1)
        find_top(1)
        make_shifts(0, (1,))
        project(2)
        project(3)
        project(4)
        find_top(2)
        find_top(3)
        regroup_v(0, 0, nc.vector.tensor_copy)
        regroup_v(0, 1, nc.vector.tensor_copy)
        for j in range(PACK):
            load_x(LOAD_AHEAD, j)
        last = GROUPS - 1
        for t in range(BANKS + 1):
            group, phase = divmod(t, PACK)
            chunk, hh = divmod(group, HALVES)
            following = chunk + 1
            step = t % BANKS_PER_CHUNK
            done = group - 1
            scaling = 0 <= done < last - 1
            if group == last and phase == 0:
                invert_sums(last - 1, 0, HALF)
            if following < CHUNKS:
                for j in {0: (0,), 1: (1, 2), 3: (3,)}.get(step, ()):
                    if t >= PACK or j >= 0:
                        transpose_x(following, j)
            if step - 4 in {1: (4, 6), 3: (6, 8)} and following < CHUNKS:
                multiply_v(following, *{1: (4, 6), 3: (6, 8)}[step - 4])
            if 5 <= t + TENSOR_LEAD < BANKS:
                project(t + TENSOR_LEAD)
            if scaling and phase in (1, 3):
                unit = 2 if phase == 1 else 3
                if phase == 1:
                    invert_sums(done, 0, 3)
                else:
                    invert_sums(done, 3, 4)
                scale_p(done, unit, nc.gpsimd, 0, GC)
            if phase in {1: (2, 3, 0), 3: (1, 2, 0)}:
                d, unit_, cond = {1: (2, 3, 0), 3: (1, 2, 0)}[phase]
                if 0 <= group - d < last - 1:
                    scale_p(group - d, unit_, nc.vector, GC, DH)
            if phase % 2 == 1:
                for bank in (t + VECTOR_LEAD, t + VECTOR_LEAD + 1):
                    if 4 <= bank < BANKS:
                        find_top(bank)
            if scaling and phase == 1:
                scale_p(done, 0, nc.vector)
            if scaling and phase == 2 and (done, 1) not in {}.values():
                scale_p(done, 1, nc.vector)
            if not {1: (2, 3, 0), 3: (1, 2, 0)} and scaling and phase in (1, 3) and GC < DH:
                scale_p(done, unit, nc.vector, GC, DH)
            if phase == 2 and 0 <= group - 2 < last - 1:
                quantise_p(group - 2, 0, HALF)
            if group == last and phase == 0:
                for h in range(HALF):
                    if (last - 1, h) not in {}.values():
                        scale_p(last - 1, h, nc.vector)
            for head in FIRST_V.get(t, ()):
                regroup_v(0, head, nc.vector.tensor_copy)
            if step in (4,) and following < CHUNKS:
                regroup_v(following, (4,).index(step), nc.vector.tensor_copy)
            if step == 7 and 0 <= chunk < 7:
                quantise_v(chunk)
            if group < last and t >= 0:
                for h in range(HALF):
                    exponentials(group, phase, h)
            if group == last:
                for j in range(PACK):
                    exponentials(group, j, phase)
            if t in {}:
                scale_p_on_scalar({}[t][0], {}[t][1])
            if phase % 2 == 1 and group < last:
                make_shifts((t + 1) // 2, (0, 1))
                if t == BANKS - PACK - 1:
                    make_shifts((t + 3) // 2, (0, 1))
            if hh == 0 and following < CHUNKS:
                copy_x(following, phase)
            if hh == 1 and following < CHUNKS:
                for head in {0: [], 1: [1], 2: [2], 3: [3]}[phase]:
                    regroup_v(following, head, nc.scalar.copy)
                if phase - 0 in {1: (4, 6), 3: (6, 8)}:
                    copy_v(following, *{1: (4, 6), 3: (6, 8)}[phase - 0])
            if following < CHUNKS:
                for j in QX.get(step, ()):
                    quantise_x(following, j)
            if phase == PACK - 1 and hh == 0 and following + LOAD_AHEAD < CHUNKS:
                for j in range(PACK):
                    load_x(following + LOAD_AHEAD, j)
            if step == 7 and 0 <= chunk < CHUNKS - LOAD_AHEAD:
                for pair in range(PACK):
                    load_v(chunk + LOAD_AHEAD, pair)
            for i in range(B * HALVES // 2):
                if t == (57, 59)[i]:
                    summarise(0, i * HALF, (i + 1) * HALF)
                if t == (57, 59)[i] + 1:
                    store(0, i * HALF, (i + 1) * HALF)
            if t == BANKS:
                quantise_v(CHUNKS - 1)
                invert_sums(last, 3, 4)
                invert_sums(last, 2, 3)
                invert_sums(last, 0, 1)
                scale_p_on_scalar(last, 3)
                quantise_p(last - 1, 0, HALF)
                summarise(B - 1, 0, HALF)
                scale_p(last, 0, nc.vector)
                invert_sums(last, 1, 2)
                scale_p(last, 1, nc.vector)
                quantise_p(last, 0, 1)
                summarise(B - 1, HALF + 0, HALF + 1)
                scale_p(last, 2, nc.vector)
                store(B - 1, 0, HALF)
                quantise_p(last, 1, 2)
                summarise(B - 1, HALF + 1, HALF + 2)
                store(B - 1, HALF + 0, HALF + 1)
                quantise_p(last, 3, 4)
                summarise(B - 1, HALF + 3, HALF + 4)
                store(B - 1, HALF + 1, HALF + 2)
                quantise_p(last, 2, 3)
                summarise(B - 1, HALF + 2, HALF + 3)
                store(B - 1, HALF + 3, HALF + 4)
                store(B - 1, HALF + 2, HALF + 3)
